import numpy as np
import ml_dtypes


def mxq(x, axis, fmt="e4m3"):
    dtype, down = {"e4m3": (ml_dtypes.float8_e4m3fn, 7), "e5m2": (ml_dtypes.float8_e5m2, 14)}[fmt]
    v = np.moveaxis(np.asarray(x, np.float32).astype(ml_dtypes.bfloat16).astype(np.float64), axis, -1)
    blocks = v.reshape(v.shape[:-1] + (-1, 32))
    amax = np.abs(blocks).max(-1, keepdims=True)
    byte = np.maximum(np.where(amax > 0, np.frexp(amax)[1] - 1 + 127, 0) - down, 1)
    scale = np.exp2(byte - 127.0)
    codes = (blocks / scale).astype(np.float32).astype(dtype).astype(np.float64)
    return np.moveaxis((codes * scale).reshape(v.shape), -1, axis)


WIDE = False


def mx_kscale(k):
    if not WIDE:
        return np.ones(k)
    levels = np.array([10, -10, 5, -5, 0])
    a = np.random.permutation(np.resize(levels, k // 512 * 4)).reshape(k // 512, 4)
    idx = np.arange(k)
    return np.exp2(a[idx // 512, idx % 128 // 32])


BF16 = ml_dtypes.bfloat16


def bf(x):
    return np.asarray(x, np.float32).astype(BF16)


def f64(x):
    return np.asarray(x).astype(np.float64)


B, S, D, H, WIN = 8, 512, 512, 2, 128
DK = D // H
NB = S // WIN


def window_softmax(scores):
    causal = np.tril(np.ones((S, S), dtype=bool)).reshape(1, 1, NB, WIN, NB, WIN)
    sc = np.where(causal, scores.reshape(B, H, NB, WIN, NB, WIN), -np.inf)
    m = sc.max(-1, keepdims=True)
    e = np.exp(sc - np.where(np.isfinite(m), m, 0.0))
    e = np.where(causal, e, 0.0)
    denom = e.sum(-1, keepdims=True)
    return (e / np.where(denom == 0.0, 1.0, denom)).reshape(B, H, S, S)


def setup_inputs():
    t = mx_kscale(D)
    return {"q": bf(np.random.standard_normal((B, H, S, DK)) * 2.5),
            "k": bf(np.random.standard_normal((B, H, S, DK)) * 2.5),
            "v": bf(np.random.standard_normal((B, H, S, DK)) * 3.0 * t.reshape(H, 1, DK)),
            "Wo_w": bf(np.random.standard_normal((D, D)) * 4.0 / np.sqrt(D) / t),
            "Wo_b": bf(np.random.standard_normal(D) * 0.1)}


def reference(q, k, v, Wo_w, Wo_b):
    scores = f64(q) @ f64(k).transpose(0, 1, 3, 2) / np.sqrt(DK)
    p = window_softmax(scores)
    e = np.exp(p)
    a = (mxq(e, 3, "e4m3") @ mxq(f64(v), 2, "e4m3")) / e.sum(-1, keepdims=True)
    a = a.transpose(0, 2, 1, 3).reshape(B, S, D)
    return (mxq(a, 2, "e4m3") @ mxq(f64(Wo_w), 1, "e4m3").T) + f64(Wo_b)

@@ -1,0 +1,344 @@
+from contextlib import ExitStack
+
+import concourse.mybir as mybir
+from concourse.masks import make_identity
+
+BF16 = mybir.dt.bfloat16
+F32 = mybir.dt.float32
+U32 = mybir.dt.uint32
+U8 = mybir.dt.uint8
+FP8X4 = mybir.dt.float8_e4m3fn_x4
+ALU = mybir.AluOpType
+ACT = mybir.ActivationFunctionType
+AXIS_X = mybir.AxisListType.X
+
+B, H, S, DK = 8, 2, 512, 256
+D = H * DK
+P = 128
+NB = S // P
+NC = DK // P
+N_HEADS = B * H
+MASKED = 1.0e30
+
+FLOPS = 2 * B * H * S * S * DK * 2 + 2 * B * S * D * D
+
+
+def tile_multiheadattention_pa_t_kernel(tc, q, k, v, Wo_w, Wo_b, out):
+    nc = tc.nc
+    with ExitStack() as ctx:
+        const = ctx.enter_context(tc.tile_pool(name="const", bufs=1))
+        inputs = ctx.enter_context(tc.tile_pool(name="inputs", bufs=B))
+        heads = ctx.enter_context(tc.tile_pool(name="heads", bufs=2))
+        units = ctx.enter_context(tc.tile_pool(name="units", bufs=3))
+        stats = ctx.enter_context(tc.tile_pool(name="stats", bufs=4))
+        psum_tr = ctx.enter_context(tc.psum_pool(name="psum_tr", bufs=4))
+        psum_sc = ctx.enter_context(tc.psum_pool(name="psum_sc", bufs=2))
+        psum_mx = ctx.enter_context(tc.psum_pool(name="psum_mx", bufs=2))
+
+        q_sb, k_sb, v_sb = [], [], []
+        wo_sb = const.tile([P, NB, D], BF16)
+        bias_bc = const.tile([P, D], BF16)
+        for b in range(B):
+            q_b = inputs.tile([P, H, NB, DK], BF16)
+            k_b = inputs.tile([P, H, NB, DK], BF16)
+            v_b = inputs.tile([P, H, NB, DK], BF16)
+            nc.sync.dma_start(out=q_b[:], in_=q[b].rearrange("h (n p) d -> p h n d", p=P))
+            nc.sync.dma_start(out=k_b[:], in_=k[b].rearrange("h (n p) d -> p h n d", p=P))
+            nc.sync.dma_start(out=v_b[:], in_=v[b].rearrange("h (t p) c -> p h t c", p=P))
+            if b == 0:
+                nc.sync.dma_start(out=wo_sb[:], in_=Wo_w.rearrange("(n p) f -> p n f", p=P))
+                nc.sync.dma_start(out=bias_bc[:], in_=Wo_b.partition_broadcast(P))
+            q_sb.append(q_b)
+            k_sb.append(k_b)
+            v_sb.append(v_b)
+
+        ident = const.tile([P, P], BF16)
+        make_identity(nc, ident[:])
+        neg_ident = const.tile([P, P], BF16)
+        nc.vector.tensor_scalar(out=neg_ident[:], in0=ident[:], scalar1=-1.0 / 16.0, scalar2=None, op0=ALU.mult)
+        mask_f32 = const.tile([P, P], F32)
+        nc.gpsimd.memset(mask_f32[:], 0.0)
+        nc.gpsimd.affine_select(
+            out=mask_f32[:], in_=mask_f32[:], pattern=[[-1, P]], compare_op=ALU.is_ge,
+            fill=MASKED, base=0, channel_multiplier=1,
+        )
+        mask = const.tile([P, P], BF16)
+        nc.vector.tensor_copy(out=mask[:], in_=mask_f32[:])
+
+        e_grouped, e_sums, e_codes, e_scales = [], [], [], []
+        for parity in range(2):
+            e_grouped_x = const.tile([P, NB, P, NB], BF16, name="e_grouped_%d" % parity, align_bytes=64)
+            e_sums_x = const.tile([P, NB, NB], F32, name="e_sums_%d" % parity)
+            e_codes_x = const.tile([P, S], U32, name="e_codes_%d" % parity, align_bytes=64)
+            e_scales_x = const.tile([P, S], U8, name="e_scales_%d" % parity, align_bytes=64)
+            nc.vector.memset(e_grouped_x[:], 1.0)
+            nc.vector.memset(e_sums_x[:], float(P))
+            e_grouped.append(e_grouped_x)
+            e_sums.append(e_sums_x)
+            e_codes.append(e_codes_x)
+            e_scales.append(e_scales_x)
+
+        wo_codes = const.tile([P, D], U32, align_bytes=64)
+        wo_scales = const.tile([P, D], U8, align_bytes=64)
+
+        qT_psum, kT_psum, qT, kT, v_grouped, v_codes, v_scales, row_inv, av = {}, {}, {}, {}, {}, {}, {}, {}, {}
+        scores, shift, win_sum, win_inv, ex, e_bf, eT = {}, {}, {}, {}, {}, {}, {}
+        a_bf, rows_T, rows_grouped, a_codes, a_scales, proj, o_sb = {}, {}, {}, {}, {}, {}, {}
+
+        def transpose_q(i):
+            b, h = divmod(i, H)
+            qT_ps = psum_tr.tile([P, NC, S], BF16, tag="tr")
+            for n in range(NB):
+                for c in range(NC):
+                    nc.tensor.matmul(
+                        out=qT_ps[:, c, n * P : (n + 1) * P], lhsT=q_sb[b][:, h, n, c * P : (c + 1) * P],
+                        rhs=neg_ident[:], start=True, stop=True,
+                    )
+            qT_psum[i] = qT_ps
+
+        def transpose_k(i):
+            b, h = divmod(i, H)
+            kT_ps = psum_tr.tile([P, NC, S], BF16, tag="tr")
+            for n in range(NB):
+                for c in range(NC):
+                    nc.tensor.transpose(
+                        out=kT_ps[:, c, n * P : (n + 1) * P], in_=k_sb[b][:, h, n, c * P : (c + 1) * P],
+                        identity=ident[:],
+                    )
+            kT_psum[i] = kT_ps
+
+        def copy_qT(i):
+            qT_sb = heads.tile([P, NC, S], BF16, tag="qT")
+            nc.vector.tensor_copy(out=qT_sb[:], in_=qT_psum[i][:])
+            qT[i] = qT_sb
+
+        def copy_kT(i):
+            kT_sb = heads.tile([P, NC, S], BF16, tag="kT")
+            nc.vector.tensor_copy(out=kT_sb[:], in_=kT_psum[i][:])
+            kT[i] = kT_sb
+
+        def group_v(i):
+            b, h = divmod(i, H)
+            v_g = heads.tile([P, DK, NB], BF16, tag="v_grouped", align_bytes=64)
+            nc.vector.tensor_copy(out=v_g[:], in_=v_sb[b][:, h].rearrange("p t c -> p c t"))
+            v_grouped[i] = v_g
+
+        def quantise_v(i):
+            v_c = heads.tile([P, DK], U32, tag="v_codes", align_bytes=64)
+            v_s = heads.tile([P, DK], U8, tag="v_scales", align_bytes=64)
+            nc.vector.quantize_mx(
+                out=v_c[:].bitcast(FP8X4), scales=v_s[:], in_=v_grouped[i][:].rearrange("p c t -> p (c t)")
+            )
+            v_codes[i], v_scales[i] = v_c, v_s
+
+        def invert_row_sums(i):
+            row_sum = stats.tile([P, NB], F32, tag="row_sum")
+            nc.vector.tensor_reduce(out=row_sum[:], in_=e_sums[i % 2][:], axis=AXIS_X, op=ALU.add)
+            row_inv_i = stats.tile([P, NB], F32, tag="row_inv")
+            nc.vector.reciprocal(out=row_inv_i[:], in_=row_sum[:])
+            row_inv[i] = row_inv_i
+
+        def e_times_v(i):
+            for pair in range(NB // 2):
+                av_ps = psum_mx.tile([P, 2, DK], F32, tag="mx")
+                for r in range(2):
+                    cols = slice((2 * pair + r) * P, (2 * pair + r + 1) * P)
+                    nc.tensor.matmul_mx(
+                        out=av_ps[:, r, :],
+                        lhsT=e_codes[i % 2][:, cols].bitcast(FP8X4), lhsT_scale=e_scales[i % 2][:, cols],
+                        rhs=v_codes[i][:].bitcast(FP8X4), rhs_scale=v_scales[i][:],
+                        start=True, stop=True,
+                    )
+                av[(i, pair)] = av_ps
+
+        def divide_by_row_sums(i):
+            b, h = divmod(i, H)
+            if h == 0:
+                a_b = heads.tile([P, NB, D], BF16, tag="a_bf")
+                a_bf[b] = a_b
+            for n in range(NB):
+                nc.scalar.activation(
+                    out=a_bf[b][:, n, h * DK : (h + 1) * DK], in_=av[(i, n // 2)][:, n % 2, :],
+                    func=ACT.Copy, scale=row_inv[i][:, n : n + 1],
+                )
+
+        def negated_scores(i, n):
+            keys = (n + 1) * P
+            diag = slice(n * P, (n + 1) * P)
+            sc = psum_sc.tile([P, S], F32, tag="sc")
+            nc.tensor.matmul(out=sc[:, :keys], lhsT=qT[i][:, 0, diag], rhs=kT[i][:, 0, :keys], start=True, stop=False)
+            nc.tensor.matmul(out=sc[:, diag], lhsT=ident[:], rhs=mask[:], start=False, stop=False)
+            nc.tensor.matmul(out=sc[:, :keys], lhsT=qT[i][:, 1, diag], rhs=kT[i][:, 1, :keys], start=False, stop=True)
+            scores[(i, n)] = sc
+
+        def window_minima(i, n):
+            sh = stats.tile([P, NB], F32, tag="shift")
+            nc.vector.tensor_reduce(
+                out=sh[:, : n + 1], in_=scores[(i, n)][:, : (n + 1) * P].rearrange("p (w j) -> p w j", j=P),
+                axis=AXIS_X, op=ALU.min,
+            )
+            shift[(i, n)] = sh
+
+        def first_exp(i, n):
+            ex_u = units.tile([P, NB, P], F32, tag="ex")
+            ws = stats.tile([P, NB], F32, tag="win_sum")
+            for w in range(n + 1):
+                nc.scalar.activation(
+                    out=ex_u[:, w, :], in_=scores[(i, n)][:, w * P : (w + 1) * P], func=ACT.Exp,
+                    scale=-1.0, bias=shift[(i, n)][:, w : w + 1], accum_out=ws[:, w : w + 1],
+                )
+            ex[(i, n)], win_sum[(i, n)] = ex_u, ws
+
+        def invert_window_sums(i, n):
+            wi = stats.tile([P, NB], F32, tag="win_inv")
+            nc.vector.reciprocal(out=wi[:, : n + 1], in_=win_sum[(i, n)][:, : n + 1])
+            win_inv[(i, n)] = wi
+
+        def second_exp(i, n):
+            e_u = units.tile([P, NB, P], BF16, tag="e_bf")
+            for w in range(n + 1):
+                nc.scalar.activation(
+                    out=e_u[:, w, :], in_=ex[(i, n)][:, w, :], func=ACT.Exp,
+                    scale=win_inv[(i, n)][:, w : w + 1], accum_out=e_sums[i % 2][:, n, w : w + 1],
+                )
+            e_bf[(i, n)] = e_u
+
+        def transpose_e(i, n):
+            eT_ps = psum_tr.tile([P, NB, P], BF16, tag="tr")
+            for w in range(n + 1):
+                nc.tensor.transpose(out=eT_ps[:, w, :], in_=e_bf[(i, n)][:, w, :], identity=ident[:])
+            eT[(i, n)] = eT_ps
+
+        def group_e(i, n):
+            nc.scalar.copy(
+                out=e_grouped[i % 2][:, n, :, : n + 1], in_=eT[(i, n)][:, : n + 1, :].rearrange("p t j -> p j t")
+            )
+
+        def quantise_e(i, n):
+            cols = slice(n * P, (n + 1) * P)
+            nc.vector.quantize_mx(
+                out=e_codes[i % 2][:, cols].bitcast(FP8X4), scales=e_scales[i % 2][:, cols],
+                in_=e_grouped[i % 2][:, n].rearrange("p j t -> p (j t)"),
+            )
+
+        def transpose_rows(g, n):
+            rows = wo_sb if g == 0 else a_bf[g - 1]
+            rT_ps = psum_tr.tile([P, NB, P], BF16, tag="tr")
+            for t in range(NB):
+                nc.tensor.transpose(out=rT_ps[:, t, :], in_=rows[:, n, t * P : (t + 1) * P], identity=ident[:])
+            rows_T[(g, n)] = rT_ps
+
+        def group_rows(g, n):
+            r_g = units.tile([P, P, NB], BF16, tag="rows_grouped", align_bytes=64)
+            nc.vector.tensor_copy(out=r_g[:], in_=rows_T[(g, n)][:].rearrange("p t j -> p j t"))
+            rows_grouped[(g, n)] = r_g
+
+        def quantise_rows(g, n):
+            if g > 0 and n == 0:
+                a_c = heads.tile([P, S], U32, tag="a_codes", align_bytes=64)
+                a_s = heads.tile([P, S], U8, tag="a_scales", align_bytes=64)
+                a_codes[g], a_scales[g] = a_c, a_s
+            codes, scales = (wo_codes, wo_scales) if g == 0 else (a_codes[g], a_scales[g])
+            cols = slice(n * P, (n + 1) * P)
+            nc.vector.quantize_mx(
+                out=codes[:, cols].bitcast(FP8X4), scales=scales[:, cols],
+                in_=rows_grouped[(g, n)][:].rearrange("p j t -> p (j t)"),
+            )
+
+        def project(g, n):
+            cols = slice(n * P, (n + 1) * P)
+            o_ps = psum_mx.tile([P, D], F32, tag="mx")
+            nc.tensor.matmul_mx(
+                out=o_ps[:],
+                lhsT=a_codes[g][:, cols].bitcast(FP8X4), lhsT_scale=a_scales[g][:, cols],
+                rhs=wo_codes[:].bitcast(FP8X4), rhs_scale=wo_scales[:],
+                start=True, stop=True,
+            )
+            proj[(g, n)] = o_ps
+
+        def add_bias_and_store(g, n):
+            if n == 0:
+                o_b = heads.tile([P, NB, D], F32, tag="o_sb")
+                o_sb[g] = o_b
+            nc.vector.tensor_tensor(out=o_sb[g][:, n, :], in0=proj[(g, n)][:], in1=bias_bc[:], op=ALU.add)
+            if n == NB - 1:
+                nc.sync.dma_start(out=out[g - 1].rearrange("(n p) o -> p n o", p=P), in_=o_sb[g][:])
+
+        n_units = N_HEADS * NB
+
+        def unit(step):
+            return divmod(step, NB) if 0 <= step < n_units else None
+
+        def rows_block(step):
+            g, n = divmod(step, H * NB)
+            return (g, n) if 0 <= g <= B and n < NB else None
+
+        DIVIDE_LAG = 8
+        ROWS_LAG = DIVIDE_LAG
+
+        transpose_q(0)
+        transpose_k(0)
+        copy_qT(0)
+        copy_kT(0)
+        for step in range(n_units + ROWS_LAG + NB + 5):
+            u = unit(step - 2)
+            if u:
+                invert_window_sums(*u)
+            u = unit(step - 1)
+            if u:
+                first_exp(*u)
+            u = unit(step - 2)
+            if u:
+                second_exp(*u)
+            u = unit(step)
+            if u:
+                negated_scores(*u)
+                window_minima(*u)
+            u = unit(step - 3)
+            if u:
+                transpose_e(*u)
+            u = unit(step - 4)
+            if u:
+                group_e(*u)
+            u = unit(step - 5)
+            if u:
+                quantise_e(*u)
+
+            u = unit(step)
+            if u and u[0] + 1 < N_HEADS:
+                if u[1] == 0:
+                    transpose_q(u[0] + 1)
+                if u[1] == 1:
+                    transpose_k(u[0] + 1)
+                    copy_qT(u[0] + 1)
+                if u[1] == 2:
+                    copy_kT(u[0] + 1)
+            if u and u[1] == 2:
+                group_v(u[0])
+            if u and u[1] == 3:
+                quantise_v(u[0])
+            u = unit(step - 3)
+            if u and u[1] == NB - 1:
+                invert_row_sums(u[0])
+            u = unit(step - 6)
+            if u and u[1] == NB - 1:
+                e_times_v(u[0])
+            u = unit(step - 7)
+            if u and u[1] == NB - 1:
+                divide_by_row_sums(u[0])
+
+            r = rows_block(step - ROWS_LAG)
+            if r:
+                transpose_rows(*r)
+            r = rows_block(step - ROWS_LAG - 1)
+            if r:
+                group_rows(*r)
+            r = rows_block(step - ROWS_LAG - 2)
+            if r:
+                quantise_rows(*r)
+            r = rows_block(step - ROWS_LAG - 3)
+            if r and r[0] > 0:
+                project(*r)
+            r = rows_block(step - ROWS_LAG - 4)
+            if r and r[0] > 0:
+                add_bias_and_store(*r)

@@ -42,9 +42,13 @@ def tile_multiheadattention_pa_t_kernel(tc, q, k, v, Wo_w, Wo_b, out):
             q_b = inputs.tile([P, H, NB, DK], BF16)
             k_b = inputs.tile([P, H, NB, DK], BF16)
             v_b = inputs.tile([P, H, NB, DK], BF16)
-            nc.sync.dma_start(out=q_b[:], in_=q[b].rearrange("h (n p) d -> p h n d", p=P))
-            nc.sync.dma_start(out=k_b[:], in_=k[b].rearrange("h (n p) d -> p h n d", p=P))
-            nc.sync.dma_start(out=v_b[:], in_=v[b].rearrange("h (t p) c -> p h t c", p=P))
+            for h in range(H):
+                nc.sync.dma_start(out=q_b[:, h], in_=q[b, h].rearrange("(n p) d -> p n d", p=P))
+                nc.sync.dma_start(out=k_b[:, h], in_=k[b, h].rearrange("(n p) d -> p n d", p=P))
+            nc.sync.dma_start(
+                out=v_b[:].rearrange("p h (u c) d -> p h u c d", u=2),
+                in_=v[b].rearrange("h (u p c) d -> p h u c d", u=2, c=2),
+            )
             if b == 0:
                 nc.sync.dma_start(out=wo_sb[:], in_=Wo_w.rearrange("(n p) f -> p n f", p=P))
                 nc.sync.dma_start(out=bias_bc[:], in_=Wo_b.partition_broadcast(P))
@@ -54,6 +58,8 @@ def tile_multiheadattention_pa_t_kernel(tc, q, k, v, Wo_w, Wo_b, out):
 
         ident = const.tile([P, P], BF16)
         make_identity(nc, ident[:])
+        ident_f32 = const.tile([P, P], F32)
+        make_identity(nc, ident_f32[:])
         neg_ident = const.tile([P, P], BF16)
         nc.vector.tensor_scalar(out=neg_ident[:], in0=ident[:], scalar1=-1.0 / 16.0, scalar2=None, op0=ALU.mult)
         mask_f32 = const.tile([P, P], F32)
@@ -65,15 +71,17 @@ def tile_multiheadattention_pa_t_kernel(tc, q, k, v, Wo_w, Wo_b, out):
         mask = const.tile([P, P], BF16)
         nc.vector.tensor_copy(out=mask[:], in_=mask_f32[:])
 
-        e_grouped, e_sums, e_codes, e_scales = [], [], [], []
+        e_bf = []
+        for n in range(NB):
+            e_bf_n = const.tile([P, NB, P], BF16, name="e_bf_%d" % n)
+            nc.vector.memset(e_bf_n[:], 1.0)
+            e_bf.append(e_bf_n)
+        e_sums, e_codes, e_scales = [], [], []
         for parity in range(2):
-            e_grouped_x = const.tile([P, NB, P, NB], BF16, name="e_grouped_%d" % parity, align_bytes=64)
             e_sums_x = const.tile([P, NB, NB], F32, name="e_sums_%d" % parity)
             e_codes_x = const.tile([P, S], U32, name="e_codes_%d" % parity, align_bytes=64)
             e_scales_x = const.tile([P, S], U8, name="e_scales_%d" % parity, align_bytes=64)
-            nc.vector.memset(e_grouped_x[:], 1.0)
             nc.vector.memset(e_sums_x[:], float(P))
-            e_grouped.append(e_grouped_x)
             e_sums.append(e_sums_x)
             e_codes.append(e_codes_x)
             e_scales.append(e_scales_x)
@@ -82,7 +90,7 @@ def tile_multiheadattention_pa_t_kernel(tc, q, k, v, Wo_w, Wo_b, out):
         wo_scales = const.tile([P, D], U8, align_bytes=64)
 
         qT_psum, kT_psum, qT, kT, v_grouped, v_codes, v_scales, row_inv, av = {}, {}, {}, {}, {}, {}, {}, {}, {}
-        scores, shift, win_sum, win_inv, ex, e_bf, eT = {}, {}, {}, {}, {}, {}, {}
+        scores, shift, win_sum, win_inv, ex, eT, e_grouped = {}, {}, {}, {}, {}, {}, {}
         a_bf, rows_T, rows_grouped, a_codes, a_scales, proj, o_sb = {}, {}, {}, {}, {}, {}, {}
 
         def transpose_q(i):
@@ -120,14 +128,17 @@ def tile_multiheadattention_pa_t_kernel(tc, q, k, v, Wo_w, Wo_b, out):
         def group_v(i):
             b, h = divmod(i, H)
             v_g = heads.tile([P, DK, NB], BF16, tag="v_grouped", align_bytes=64)
-            nc.vector.tensor_copy(out=v_g[:], in_=v_sb[b][:, h].rearrange("p t c -> p c t"))
+            nc.vector.tensor_copy(
+                out=v_g[:].rearrange("p (d r) t -> p d t r", r=4),
+                in_=v_sb[b][:, h].rearrange("p t (d r) -> p d t r", r=4),
+            )
             v_grouped[i] = v_g
 
         def quantise_v(i):
             v_c = heads.tile([P, DK], U32, tag="v_codes", align_bytes=64)
             v_s = heads.tile([P, DK], U8, tag="v_scales", align_bytes=64)
             nc.vector.quantize_mx(
-                out=v_c[:].bitcast(FP8X4), scales=v_s[:], in_=v_grouped[i][:].rearrange("p c t -> p (c t)")
+                out=v_c[:].bitcast(FP8X4), scales=v_s[:], in_=v_grouped[i][:].rearrange("p d t -> p (d t)")
             )
             v_codes[i], v_scales[i] = v_c, v_s
 
@@ -195,42 +206,44 @@ def tile_multiheadattention_pa_t_kernel(tc, q, k, v, Wo_w, Wo_b, out):
             win_inv[(i, n)] = wi
 
         def second_exp(i, n):
-            e_u = units.tile([P, NB, P], BF16, tag="e_bf")
             for w in range(n + 1):
                 nc.scalar.activation(
-                    out=e_u[:, w, :], in_=ex[(i, n)][:, w, :], func=ACT.Exp,
+                    out=e_bf[n][:, w, :], in_=ex[(i, n)][:, w, :], func=ACT.Exp,
                     scale=win_inv[(i, n)][:, w : w + 1], accum_out=e_sums[i % 2][:, n, w : w + 1],
                 )
-            e_bf[(i, n)] = e_u
+
+        def transpose_words(rows):
+            words = rows.bitcast(F32)
+            wT_ps = psum_tr.tile([P, 2, P], F32, tag="tr")
+            for u in range(2):
+                nc.tensor.transpose(out=wT_ps[:, u, :], in_=words[:, u * P : (u + 1) * P], identity=ident_f32[:])
+            return wT_ps
 
         def transpose_e(i, n):
-            eT_ps = psum_tr.tile([P, NB, P], BF16, tag="tr")
-            for w in range(n + 1):
-                nc.tensor.transpose(out=eT_ps[:, w, :], in_=e_bf[(i, n)][:, w, :], identity=ident[:])
-            eT[(i, n)] = eT_ps
+            eT[(i, n)] = transpose_words(e_bf[n][:].rearrange("p w j -> p (w j)"))
 
         def group_e(i, n):
+            e_g = units.tile([P, NB * P], BF16, tag="e_grouped", align_bytes=64)
             nc.scalar.copy(
-                out=e_grouped[i % 2][:, n, :, : n + 1], in_=eT[(i, n)][:, : n + 1, :].rearrange("p t j -> p j t")
+                out=e_g[:].bitcast(F32).rearrange("p (j u) -> p j u", u=2), in_=eT[(i, n)][:].rearrange("p u j -> p j u")
             )
+            e_grouped[(i, n)] = e_g
 
         def quantise_e(i, n):
             cols = slice(n * P, (n + 1) * P)
             nc.vector.quantize_mx(
-                out=e_codes[i % 2][:, cols].bitcast(FP8X4), scales=e_scales[i % 2][:, cols],
-                in_=e_grouped[i % 2][:, n].rearrange("p j t -> p (j t)"),
+                out=e_codes[i % 2][:, cols].bitcast(FP8X4), scales=e_scales[i % 2][:, cols], in_=e_grouped[(i, n)][:]
             )
 
         def transpose_rows(g, n):
             rows = wo_sb if g == 0 else a_bf[g - 1]
-            rT_ps = psum_tr.tile([P, NB, P], BF16, tag="tr")
-            for t in range(NB):
-                nc.tensor.transpose(out=rT_ps[:, t, :], in_=rows[:, n, t * P : (t + 1) * P], identity=ident[:])
-            rows_T[(g, n)] = rT_ps
+            rows_T[(g, n)] = transpose_words(rows[:, n, :])
 
         def group_rows(g, n):
-            r_g = units.tile([P, P, NB], BF16, tag="rows_grouped", align_bytes=64)
-            nc.vector.tensor_copy(out=r_g[:], in_=rows_T[(g, n)][:].rearrange("p t j -> p j t"))
+            r_g = units.tile([P, NB * P], BF16, tag="rows_grouped", align_bytes=64)
+            nc.vector.tensor_copy(
+                out=r_g[:].bitcast(F32).rearrange("p (j u) -> p j u", u=2), in_=rows_T[(g, n)][:].rearrange("p u j -> p j u")
+            )
             rows_grouped[(g, n)] = r_g
 
         def quantise_rows(g, n):
@@ -242,7 +255,7 @@ def tile_multiheadattention_pa_t_kernel(tc, q, k, v, Wo_w, Wo_b, out):
             cols = slice(n * P, (n + 1) * P)
             nc.vector.quantize_mx(
                 out=codes[:, cols].bitcast(FP8X4), scales=scales[:, cols],
-                in_=rows_grouped[(g, n)][:].rearrange("p j t -> p (j t)"),
+                in_=rows_grouped[(g, n)][:],
             )
 
         def project(g, n):

@@ -38,19 +38,19 @@ def tile_multiheadattention_pa_t_kernel(tc, q, k, v, Wo_w, Wo_b, out):
         q_sb, k_sb, v_sb = [], [], []
         wo_sb = const.tile([P, NB, D], BF16)
         bias_bc = const.tile([P, D], BF16)
+        nc.sync.dma_start(out=wo_sb[:], in_=Wo_w.rearrange("(n p) f -> p n f", p=P))
         for b in range(B):
             q_b = inputs.tile([P, H, NB, DK], BF16)
             k_b = inputs.tile([P, H, NB, DK], BF16)
             v_b = inputs.tile([P, H, NB, DK], BF16)
-            for h in range(H):
-                nc.sync.dma_start(out=q_b[:, h], in_=q[b, h].rearrange("(n p) d -> p n d", p=P))
-                nc.sync.dma_start(out=k_b[:, h], in_=k[b, h].rearrange("(n p) d -> p n d", p=P))
             nc.sync.dma_start(
                 out=v_b[:].rearrange("p h (u c) d -> p h u c d", u=2),
                 in_=v[b].rearrange("h (u p c) d -> p h u c d", u=2, c=2),
             )
+            for h in range(H):
+                nc.sync.dma_start(out=q_b[:, h], in_=q[b, h].rearrange("(n p) d -> p n d", p=P))
+                nc.sync.dma_start(out=k_b[:, h], in_=k[b, h].rearrange("(n p) d -> p n d", p=P))
             if b == 0:
-                nc.sync.dma_start(out=wo_sb[:], in_=Wo_w.rearrange("(n p) f -> p n f", p=P))
                 nc.sync.dma_start(out=bias_bc[:], in_=Wo_b.partition_broadcast(P))
             q_sb.append(q_b)
             k_sb.append(k_b)
@@ -58,10 +58,14 @@ def tile_multiheadattention_pa_t_kernel(tc, q, k, v, Wo_w, Wo_b, out):
 
         ident = const.tile([P, P], BF16)
         make_identity(nc, ident[:])
+        neg_ident = const.tile([P, P], BF16)
+        nc.gpsimd.memset(neg_ident[:], 0.0)
+        nc.gpsimd.affine_select(
+            out=neg_ident[:], in_=neg_ident[:], pattern=[[-1, P]], compare_op=ALU.not_equal,
+            fill=-1.0 / 16.0, base=0, channel_multiplier=1,
+        )
         ident_f32 = const.tile([P, P], F32)
         make_identity(nc, ident_f32[:])
-        neg_ident = const.tile([P, P], BF16)
-        nc.vector.tensor_scalar(out=neg_ident[:], in0=ident[:], scalar1=-1.0 / 16.0, scalar2=None, op0=ALU.mult)
         mask_f32 = const.tile([P, P], F32)
         nc.gpsimd.memset(mask_f32[:], 0.0)
         nc.gpsimd.affine_select(
@@ -89,41 +93,9 @@ def tile_multiheadattention_pa_t_kernel(tc, q, k, v, Wo_w, Wo_b, out):
         wo_codes = const.tile([P, D], U32, align_bytes=64)
         wo_scales = const.tile([P, D], U8, align_bytes=64)
 
-        qT_psum, kT_psum, qT, kT, v_grouped, v_codes, v_scales, row_inv, av = {}, {}, {}, {}, {}, {}, {}, {}, {}
+        qkT_psum, qkT, v_grouped, v_codes, v_scales, row_inv, av = {}, {}, {}, {}, {}, {}, {}
         scores, shift, win_sum, win_inv, ex, eT, e_grouped = {}, {}, {}, {}, {}, {}, {}
-        a_bf, rows_T, rows_grouped, a_codes, a_scales, proj, o_sb = {}, {}, {}, {}, {}, {}, {}
-
-        def transpose_q(i):
-            b, h = divmod(i, H)
-            qT_ps = psum_tr.tile([P, NC, S], BF16, tag="tr")
-            for n in range(NB):
-                for c in range(NC):
-                    nc.tensor.matmul(
-                        out=qT_ps[:, c, n * P : (n + 1) * P], lhsT=q_sb[b][:, h, n, c * P : (c + 1) * P],
-                        rhs=neg_ident[:], start=True, stop=True,
-                    )
-            qT_psum[i] = qT_ps
-
-        def transpose_k(i):
-            b, h = divmod(i, H)
-            kT_ps = psum_tr.tile([P, NC, S], BF16, tag="tr")
-            for n in range(NB):
-                for c in range(NC):
-                    nc.tensor.transpose(
-                        out=kT_ps[:, c, n * P : (n + 1) * P], in_=k_sb[b][:, h, n, c * P : (c + 1) * P],
-                        identity=ident[:],
-                    )
-            kT_psum[i] = kT_ps
-
-        def copy_qT(i):
-            qT_sb = heads.tile([P, NC, S], BF16, tag="qT")
-            nc.vector.tensor_copy(out=qT_sb[:], in_=qT_psum[i][:])
-            qT[i] = qT_sb
-
-        def copy_kT(i):
-            kT_sb = heads.tile([P, NC, S], BF16, tag="kT")
-            nc.vector.tensor_copy(out=kT_sb[:], in_=kT_psum[i][:])
-            kT[i] = kT_sb
+        a_bf, rows_T, rows_grouped, a_codes, a_scales, proj = {}, {}, {}, {}, {}, {}
 
         def group_v(i):
             b, h = divmod(i, H)
@@ -173,13 +145,28 @@ def tile_multiheadattention_pa_t_kernel(tc, q, k, v, Wo_w, Wo_b, out):
                     func=ACT.Copy, scale=row_inv[i][:, n : n + 1],
                 )
 
+        def transpose_qk(i, n):
+            b, h = divmod(i, H)
+            qk_ps = psum_tr.tile([P, 2, NC, P], BF16, tag="tr")
+            for c in range(NC):
+                chunk = slice(c * P, (c + 1) * P)
+                nc.tensor.matmul(out=qk_ps[:, 0, c, :], lhsT=q_sb[b][:, h, n, chunk], rhs=neg_ident[:], start=True, stop=True)
+                nc.tensor.transpose(out=qk_ps[:, 1, c, :], in_=k_sb[b][:, h, n, chunk], identity=ident[:])
+            qkT_psum[(i, n)] = qk_ps
+
+        def copy_qkT(i, n):
+            if n == 0:
+                qkT_i = heads.tile([P, NB, 2, NC, P], BF16, tag="qkT")
+                qkT[i] = qkT_i
+            nc.vector.tensor_copy(out=qkT[i][:, n], in_=qkT_psum[(i, n)][:])
+
         def negated_scores(i, n):
             keys = (n + 1) * P
-            diag = slice(n * P, (n + 1) * P)
             sc = psum_sc.tile([P, S], F32, tag="sc")
-            nc.tensor.matmul(out=sc[:, :keys], lhsT=qT[i][:, 0, diag], rhs=kT[i][:, 0, :keys], start=True, stop=False)
-            nc.tensor.matmul(out=sc[:, diag], lhsT=ident[:], rhs=mask[:], start=False, stop=False)
-            nc.tensor.matmul(out=sc[:, :keys], lhsT=qT[i][:, 1, diag], rhs=kT[i][:, 1, :keys], start=False, stop=True)
+            by_window = sc[:, :keys].rearrange("p (w j) -> p w j", j=P)
+            nc.tensor.matmul(out=by_window, lhsT=qkT[i][:, n, 0, 0, :], rhs=qkT[i][:, : n + 1, 1, 0, :], start=True, stop=False)
+            nc.tensor.matmul(out=sc[:, n * P : keys], lhsT=ident[:], rhs=mask[:], start=False, stop=False)
+            nc.tensor.matmul(out=by_window, lhsT=qkT[i][:, n, 0, 1, :], rhs=qkT[i][:, : n + 1, 1, 1, :], start=False, stop=True)
             scores[(i, n)] = sc
 
         def window_minima(i, n):
@@ -270,12 +257,9 @@ def tile_multiheadattention_pa_t_kernel(tc, q, k, v, Wo_w, Wo_b, out):
             proj[(g, n)] = o_ps
 
         def add_bias_and_store(g, n):
-            if n == 0:
-                o_b = heads.tile([P, NB, D], F32, tag="o_sb")
-                o_sb[g] = o_b
-            nc.vector.tensor_tensor(out=o_sb[g][:, n, :], in0=proj[(g, n)][:], in1=bias_bc[:], op=ALU.add)
-            if n == NB - 1:
-                nc.sync.dma_start(out=out[g - 1].rearrange("(n p) o -> p n o", p=P), in_=o_sb[g][:])
+            o_sb = units.tile([P, D], F32, tag="o_sb")
+            nc.vector.tensor_tensor(out=o_sb[:], in0=proj[(g, n)][:], in1=bias_bc[:], op=ALU.add)
+            nc.sync.dma_start(out=out[g - 1, n * P : (n + 1) * P, :], in_=o_sb[:])
 
         n_units = N_HEADS * NB
 
@@ -289,11 +273,13 @@ def tile_multiheadattention_pa_t_kernel(tc, q, k, v, Wo_w, Wo_b, out):
         DIVIDE_LAG = 8
         ROWS_LAG = DIVIDE_LAG
 
-        transpose_q(0)
-        transpose_k(0)
-        copy_qT(0)
-        copy_kT(0)
-        for step in range(n_units + ROWS_LAG + NB + 5):
+        for step in range(-2, n_units + ROWS_LAG + NB + 5):
+            u = unit(step + 2)
+            if u:
+                transpose_qk(*u)
+            u = unit(step + 1)
+            if u:
+                copy_qkT(*u)
             u = unit(step - 2)
             if u:
                 invert_window_sums(*u)
@@ -318,14 +304,6 @@ def tile_multiheadattention_pa_t_kernel(tc, q, k, v, Wo_w, Wo_b, out):
                 quantise_e(*u)
 
             u = unit(step)
-            if u and u[0] + 1 < N_HEADS:
-                if u[1] == 0:
-                    transpose_q(u[0] + 1)
-                if u[1] == 1:
-                    transpose_k(u[0] + 1)
-                    copy_qT(u[0] + 1)
-                if u[1] == 2:
-                    copy_kT(u[0] + 1)
             if u and u[1] == 2:
                 group_v(u[0])
             if u and u[1] == 3:

@@ -18,6 +18,8 @@ P = 128
 NB = S // P
 NC = DK // P
 N_HEADS = B * H
+FIRST_DIRECT = 6
+E_BUFS = 8
 MASKED = 1.0e30
 
 FLOPS = 2 * B * H * S * S * DK * 2 + 2 * B * S * D * D
@@ -28,44 +30,50 @@ def tile_multiheadattention_pa_t_kernel(tc, q, k, v, Wo_w, Wo_b, out):
     with ExitStack() as ctx:
         const = ctx.enter_context(tc.tile_pool(name="const", bufs=1))
         inputs = ctx.enter_context(tc.tile_pool(name="inputs", bufs=B))
-        heads = ctx.enter_context(tc.tile_pool(name="heads", bufs=2))
-        units = ctx.enter_context(tc.tile_pool(name="units", bufs=3))
-        stats = ctx.enter_context(tc.tile_pool(name="stats", bufs=4))
-        psum_tr = ctx.enter_context(tc.psum_pool(name="psum_tr", bufs=4))
+        batches = ctx.enter_context(tc.tile_pool(name="batches", bufs=3))
+        blocks = ctx.enter_context(tc.tile_pool(name="blocks", bufs=3))
+        e_pool = ctx.enter_context(tc.tile_pool(name="e_pool", bufs=E_BUFS))
+        stats = ctx.enter_context(tc.tile_pool(name="stats", bufs=8))
+        psum = ctx.enter_context(tc.psum_pool(name="psum", bufs=1))
         psum_sc = ctx.enter_context(tc.psum_pool(name="psum_sc", bufs=2))
-        psum_mx = ctx.enter_context(tc.psum_pool(name="psum_mx", bufs=2))
 
         q_sb, k_sb, v_sb = [], [], []
         wo_sb = const.tile([P, NB, D], BF16)
         bias_bc = const.tile([P, D], BF16)
-        nc.sync.dma_start(out=wo_sb[:], in_=Wo_w.rearrange("(n p) f -> p n f", p=P))
-        for b in range(B):
+
+        def load_batch(b):
             q_b = inputs.tile([P, H, NB, DK], BF16)
             k_b = inputs.tile([P, H, NB, DK], BF16)
             v_b = inputs.tile([P, H, NB, DK], BF16)
+            if b == 0:
+                for n in range(NB):
+                    rows = slice(n * P, (n + 1) * P)
+                    nc.sync.dma_start(out=q_b[:, :, n], in_=q[b, :, rows, :].rearrange("h p d -> p h d"))
+                    nc.sync.dma_start(out=k_b[:, :, n], in_=k[b, :, rows, :].rearrange("h p d -> p h d"))
+            else:
+                nc.sync.dma_start(out=q_b[:].rearrange("p h n d -> p (h n) d"), in_=q[b].rearrange("h (n p) d -> p (h n) d", p=P))
+                nc.sync.dma_start(out=k_b[:].rearrange("p h n d -> p (h n) d"), in_=k[b].rearrange("h (n p) d -> p (h n) d", p=P))
             nc.sync.dma_start(
                 out=v_b[:].rearrange("p h (u c) d -> p h u c d", u=2),
                 in_=v[b].rearrange("h (u p c) d -> p h u c d", u=2, c=2),
             )
-            for h in range(H):
-                nc.sync.dma_start(out=q_b[:, h], in_=q[b, h].rearrange("(n p) d -> p n d", p=P))
-                nc.sync.dma_start(out=k_b[:, h], in_=k[b, h].rearrange("(n p) d -> p n d", p=P))
-            if b == 0:
-                nc.sync.dma_start(out=bias_bc[:], in_=Wo_b.partition_broadcast(P))
             q_sb.append(q_b)
             k_sb.append(k_b)
             v_sb.append(v_b)
 
-        ident = const.tile([P, P], BF16)
-        make_identity(nc, ident[:])
+        load_batch(0)
+        nc.sync.dma_start(out=wo_sb[:], in_=Wo_w.rearrange("(n p) f -> p n f", p=P))
+        nc.sync.dma_start(out=bias_bc[:], in_=Wo_b.partition_broadcast(P))
+        load_batch(1)
+
         neg_ident = const.tile([P, P], BF16)
         nc.gpsimd.memset(neg_ident[:], 0.0)
         nc.gpsimd.affine_select(
             out=neg_ident[:], in_=neg_ident[:], pattern=[[-1, P]], compare_op=ALU.not_equal,
             fill=-1.0 / 16.0, base=0, channel_multiplier=1,
         )
-        ident_f32 = const.tile([P, P], F32)
-        make_identity(nc, ident_f32[:])
+        ident = const.tile([P, P], BF16)
+        make_identity(nc, ident[:])
         mask_f32 = const.tile([P, P], F32)
         nc.gpsimd.memset(mask_f32[:], 0.0)
         nc.gpsimd.affine_select(
@@ -74,262 +82,310 @@ def tile_multiheadattention_pa_t_kernel(tc, q, k, v, Wo_w, Wo_b, out):
         )
         mask = const.tile([P, P], BF16)
         nc.vector.tensor_copy(out=mask[:], in_=mask_f32[:])
+        ident_f32 = const.tile([P, P], F32)
+        make_identity(nc, ident_f32[:])
 
-        e_bf = []
+        e_bf, e_sums = [], []
         for n in range(NB):
-            e_bf_n = const.tile([P, NB, P], BF16, name="e_bf_%d" % n)
-            nc.vector.memset(e_bf_n[:], 1.0)
+            e_bf_n = const.tile([P, H, NB, P], BF16, name="e_bf_%d" % n)
+            if n < NB - 1:
+                nc.vector.memset(e_bf_n[:, :, n + 1 :, :], 1.0)
             e_bf.append(e_bf_n)
-        e_sums, e_codes, e_scales = [], [], []
         for parity in range(2):
-            e_sums_x = const.tile([P, NB, NB], F32, name="e_sums_%d" % parity)
-            e_codes_x = const.tile([P, S], U32, name="e_codes_%d" % parity, align_bytes=64)
-            e_scales_x = const.tile([P, S], U8, name="e_scales_%d" % parity, align_bytes=64)
+            e_sums_x = const.tile([P, NB, H, NB], F32, name="e_sums_%d" % parity)
             nc.vector.memset(e_sums_x[:], float(P))
             e_sums.append(e_sums_x)
-            e_codes.append(e_codes_x)
-            e_scales.append(e_scales_x)
 
         wo_codes = const.tile([P, D], U32, align_bytes=64)
         wo_scales = const.tile([P, D], U8, align_bytes=64)
 
         qkT_psum, qkT, v_grouped, v_codes, v_scales, row_inv, av = {}, {}, {}, {}, {}, {}, {}
-        scores, shift, win_sum, win_inv, ex, eT, e_grouped = {}, {}, {}, {}, {}, {}, {}
+        row_inv_bc, avT = {}, {}
+        scores, shift, win_sum, win_inv, ex, eT, e_grouped, e_codes, e_scales = {}, {}, {}, {}, {}, {}, {}, {}, {}
         a_bf, rows_T, rows_grouped, a_codes, a_scales, proj = {}, {}, {}, {}, {}, {}
 
-        def group_v(i):
-            b, h = divmod(i, H)
-            v_g = heads.tile([P, DK, NB], BF16, tag="v_grouped", align_bytes=64)
+        def group_v(b, h):
+            v_g = batches.tile([P, DK, NB], BF16, tag="v_grouped", align_bytes=64)
             nc.vector.tensor_copy(
                 out=v_g[:].rearrange("p (d r) t -> p d t r", r=4),
                 in_=v_sb[b][:, h].rearrange("p t (d r) -> p d t r", r=4),
             )
-            v_grouped[i] = v_g
+            v_grouped[(b, h)] = v_g
 
-        def quantise_v(i):
-            v_c = heads.tile([P, DK], U32, tag="v_codes", align_bytes=64)
-            v_s = heads.tile([P, DK], U8, tag="v_scales", align_bytes=64)
+        def quantise_v(b, h):
+            v_c = batches.tile([P, DK], U32, tag="v_codes_%d" % h, align_bytes=64, name="v_c")
+            v_s = batches.tile([P, DK], U8, tag="v_scales_%d" % h, align_bytes=64, name="v_s")
             nc.vector.quantize_mx(
-                out=v_c[:].bitcast(FP8X4), scales=v_s[:], in_=v_grouped[i][:].rearrange("p d t -> p (d t)")
+                out=v_c[:].bitcast(FP8X4), scales=v_s[:], in_=v_grouped[(b, h)][:].rearrange("p d t -> p (d t)")
             )
-            v_codes[i], v_scales[i] = v_c, v_s
+            v_codes[(b, h)], v_scales[(b, h)] = v_c, v_s
 
-        def invert_row_sums(i):
-            row_sum = stats.tile([P, NB], F32, tag="row_sum")
-            nc.vector.tensor_reduce(out=row_sum[:], in_=e_sums[i % 2][:], axis=AXIS_X, op=ALU.add)
-            row_inv_i = stats.tile([P, NB], F32, tag="row_inv")
-            nc.vector.reciprocal(out=row_inv_i[:], in_=row_sum[:])
-            row_inv[i] = row_inv_i
+        def transpose_qk(b, n):
+            qk_ps = psum.tile([P, H, 2, NC, P], BF16, tag="qk")
+            for h in range(H):
+                for c in range(NC):
+                    chunk = slice(c * P, (c + 1) * P)
+                    nc.tensor.matmul(out=qk_ps[:, h, 0, c, :], lhsT=q_sb[b][:, h, n, chunk], rhs=neg_ident[:], start=True, stop=True)
+                    nc.tensor.transpose(out=qk_ps[:, h, 1, c, :], in_=k_sb[b][:, h, n, chunk], identity=ident[:])
+            qkT_psum[(b, n)] = qk_ps
 
-        def e_times_v(i):
-            for pair in range(NB // 2):
-                av_ps = psum_mx.tile([P, 2, DK], F32, tag="mx")
-                for r in range(2):
-                    cols = slice((2 * pair + r) * P, (2 * pair + r + 1) * P)
-                    nc.tensor.matmul_mx(
-                        out=av_ps[:, r, :],
-                        lhsT=e_codes[i % 2][:, cols].bitcast(FP8X4), lhsT_scale=e_scales[i % 2][:, cols],
-                        rhs=v_codes[i][:].bitcast(FP8X4), rhs_scale=v_scales[i][:],
-                        start=True, stop=True,
-                    )
-                av[(i, pair)] = av_ps
-
-        def divide_by_row_sums(i):
-            b, h = divmod(i, H)
-            if h == 0:
-                a_b = heads.tile([P, NB, D], BF16, tag="a_bf")
-                a_bf[b] = a_b
-            for n in range(NB):
-                nc.scalar.activation(
-                    out=a_bf[b][:, n, h * DK : (h + 1) * DK], in_=av[(i, n // 2)][:, n % 2, :],
-                    func=ACT.Copy, scale=row_inv[i][:, n : n + 1],
-                )
-
-        def transpose_qk(i, n):
-            b, h = divmod(i, H)
-            qk_ps = psum_tr.tile([P, 2, NC, P], BF16, tag="tr")
-            for c in range(NC):
-                chunk = slice(c * P, (c + 1) * P)
-                nc.tensor.matmul(out=qk_ps[:, 0, c, :], lhsT=q_sb[b][:, h, n, chunk], rhs=neg_ident[:], start=True, stop=True)
-                nc.tensor.transpose(out=qk_ps[:, 1, c, :], in_=k_sb[b][:, h, n, chunk], identity=ident[:])
-            qkT_psum[(i, n)] = qk_ps
-
-        def copy_qkT(i, n):
+        def copy_qkT(b, n):
             if n == 0:
-                qkT_i = heads.tile([P, NB, 2, NC, P], BF16, tag="qkT")
-                qkT[i] = qkT_i
-            nc.vector.tensor_copy(out=qkT[i][:, n], in_=qkT_psum[(i, n)][:])
+                qkT_b = batches.tile([P, NB, H, 2, NC, P], BF16, tag="qkT")
+                qkT[b] = qkT_b
+            (nc.vector.tensor_copy if n in (1,) else nc.scalar.copy)(out=qkT[b][:, n], in_=qkT_psum[(b, n)][:])
 
-        def negated_scores(i, n):
+        def negated_scores(b, n, h):
             keys = (n + 1) * P
             sc = psum_sc.tile([P, S], F32, tag="sc")
             by_window = sc[:, :keys].rearrange("p (w j) -> p w j", j=P)
-            nc.tensor.matmul(out=by_window, lhsT=qkT[i][:, n, 0, 0, :], rhs=qkT[i][:, : n + 1, 1, 0, :], start=True, stop=False)
+            nc.tensor.matmul(out=by_window, lhsT=qkT[b][:, n, h, 0, 0, :], rhs=qkT[b][:, : n + 1, h, 1, 0, :], start=True, stop=False)
             nc.tensor.matmul(out=sc[:, n * P : keys], lhsT=ident[:], rhs=mask[:], start=False, stop=False)
-            nc.tensor.matmul(out=by_window, lhsT=qkT[i][:, n, 0, 1, :], rhs=qkT[i][:, : n + 1, 1, 1, :], start=False, stop=True)
-            scores[(i, n)] = sc
+            nc.tensor.matmul(out=by_window, lhsT=qkT[b][:, n, h, 0, 1, :], rhs=qkT[b][:, : n + 1, h, 1, 1, :], start=False, stop=True)
+            scores[(b, n, h)] = sc
 
-        def window_minima(i, n):
+        def window_minima(b, n, h):
             sh = stats.tile([P, NB], F32, tag="shift")
             nc.vector.tensor_reduce(
-                out=sh[:, : n + 1], in_=scores[(i, n)][:, : (n + 1) * P].rearrange("p (w j) -> p w j", j=P),
+                out=sh[:, : n + 1], in_=scores[(b, n, h)][:, : (n + 1) * P].rearrange("p (w j) -> p w j", j=P),
                 axis=AXIS_X, op=ALU.min,
             )
-            shift[(i, n)] = sh
+            shift[(b, n, h)] = sh
 
-        def first_exp(i, n):
-            ex_u = units.tile([P, NB, P], F32, tag="ex")
-            ws = stats.tile([P, NB], F32, tag="win_sum")
+        def first_exp(b, n, h):
+            if h == 0:
+                ex_n = blocks.tile([P, H, NB, P], F32, tag="ex")
+                ws = stats.tile([P, H, NB], F32, tag="win_sum")
+                ex[(b, n)], win_sum[(b, n)] = ex_n, ws
             for w in range(n + 1):
                 nc.scalar.activation(
-                    out=ex_u[:, w, :], in_=scores[(i, n)][:, w * P : (w + 1) * P], func=ACT.Exp,
-                    scale=-1.0, bias=shift[(i, n)][:, w : w + 1], accum_out=ws[:, w : w + 1],
+                    out=ex[(b, n)][:, h, w, :], in_=scores[(b, n, h)][:, w * P : (w + 1) * P], func=ACT.Exp,
+                    scale=-1.0, bias=shift[(b, n, h)][:, w : w + 1], accum_out=win_sum[(b, n)][:, h, w : w + 1],
                 )
-            ex[(i, n)], win_sum[(i, n)] = ex_u, ws
 
-        def invert_window_sums(i, n):
-            wi = stats.tile([P, NB], F32, tag="win_inv")
-            nc.vector.reciprocal(out=wi[:, : n + 1], in_=win_sum[(i, n)][:, : n + 1])
-            win_inv[(i, n)] = wi
+        def invert_window_sums(b, n):
+            wi = stats.tile([P, H, NB], F32, tag="win_inv")
+            nc.vector.reciprocal(out=wi[:, :, : n + 1], in_=win_sum[(b, n)][:, :, : n + 1])
+            win_inv[(b, n)] = wi
 
-        def second_exp(i, n):
+        def second_exp(b, n, h):
             for w in range(n + 1):
                 nc.scalar.activation(
-                    out=e_bf[n][:, w, :], in_=ex[(i, n)][:, w, :], func=ACT.Exp,
-                    scale=win_inv[(i, n)][:, w : w + 1], accum_out=e_sums[i % 2][:, n, w : w + 1],
+                    out=e_bf[n][:, h, w, :], in_=ex[(b, n)][:, h, w, :], func=ACT.Exp,
+                    scale=win_inv[(b, n)][:, h, w : w + 1], accum_out=e_sums[b % 2][:, n, h, w : w + 1],
                 )
 
-        def transpose_words(rows):
+        def invert_row_sums(b, n):
+            if b >= FIRST_DIRECT:
+                row_sum = stats.tile([P, H], F32, tag="row_sum")
+                nc.vector.tensor_reduce(out=row_sum[:], in_=e_sums[b % 2][:, n], axis=AXIS_X, op=ALU.add)
+                row_inv_n = stats.tile([P, H], F32, tag="row_inv")
+                nc.vector.reciprocal(out=row_inv_n[:], in_=row_sum[:])
+                row_inv[(b, n)] = row_inv_n
+            elif n == NB - 1:
+                row_sum_b = stats.tile([P, NB, H], F32, tag="row_sum_b")
+                nc.vector.tensor_reduce(out=row_sum_b[:], in_=e_sums[b % 2][:], axis=AXIS_X, op=ALU.add)
+                row_inv_b = stats.tile([P, NB, H], F32, tag="row_inv_b")
+                nc.vector.reciprocal(out=row_inv_b[:], in_=row_sum_b[:])
+                parked = out[b, S - 2 : S, :]
+                nc.sync.dma_start(out=parked.rearrange("r (p x) -> (r p) x", x=NB * H), in_=row_inv_b[:].rearrange("p n h -> p (n h)"))
+                bc = batches.tile([P, P, NB, H], F32, tag="row_inv_bc")
+                nc.sync.dma_start(
+                    out=bc[:].rearrange("p j n h -> p (j n h)"), in_=parked.rearrange("r f -> (r f)").partition_broadcast(P)
+                )
+                row_inv_bc[b] = bc
+
+        def transpose_words(out_ps, rows):
             words = rows.bitcast(F32)
-            wT_ps = psum_tr.tile([P, 2, P], F32, tag="tr")
             for u in range(2):
-                nc.tensor.transpose(out=wT_ps[:, u, :], in_=words[:, u * P : (u + 1) * P], identity=ident_f32[:])
-            return wT_ps
+                nc.tensor.transpose(out=out_ps[:, u, :], in_=words[:, u * P : (u + 1) * P], identity=ident_f32[:])
 
-        def transpose_e(i, n):
-            eT[(i, n)] = transpose_words(e_bf[n][:].rearrange("p w j -> p (w j)"))
+        def transpose_e(b, n):
+            eT_ps = psum.tile([P, H, 2, P], F32, tag="e")
+            for h in range(H):
+                transpose_words(eT_ps[:, h], e_bf[n][:, h].rearrange("p w j -> p (w j)"))
+            eT[(b, n)] = eT_ps
 
-        def group_e(i, n):
-            e_g = units.tile([P, NB * P], BF16, tag="e_grouped", align_bytes=64)
+        def group_e(b, n):
+            e_g = blocks.tile([P, H * NB * P], BF16, tag="e_grouped", align_bytes=64)
             nc.scalar.copy(
-                out=e_g[:].bitcast(F32).rearrange("p (j u) -> p j u", u=2), in_=eT[(i, n)][:].rearrange("p u j -> p j u")
+                out=e_g[:].bitcast(F32).rearrange("p (h j u) -> p h j u", h=H, u=2),
+                in_=eT[(b, n)][:].rearrange("p h u j -> p h j u"),
             )
-            e_grouped[(i, n)] = e_g
+            e_grouped[(b, n)] = e_g
 
-        def quantise_e(i, n):
-            cols = slice(n * P, (n + 1) * P)
-            nc.vector.quantize_mx(
-                out=e_codes[i % 2][:, cols].bitcast(FP8X4), scales=e_scales[i % 2][:, cols], in_=e_grouped[(i, n)][:]
-            )
+        def quantise_e(b, n):
+            e_c = e_pool.tile([P, H * P], U32, tag="e_codes", align_bytes=64)
+            e_s = e_pool.tile([P, H * P], U8, tag="e_scales", align_bytes=64)
+            nc.vector.quantize_mx(out=e_c[:].bitcast(FP8X4), scales=e_s[:], in_=e_grouped[(b, n)][:])
+            e_codes[(b, n)], e_scales[(b, n)] = e_c, e_s
 
-        def transpose_rows(g, n):
-            rows = wo_sb if g == 0 else a_bf[g - 1]
-            rows_T[(g, n)] = transpose_words(rows[:, n, :])
+        def e_times_v(b, n):
+            if b >= FIRST_DIRECT:
+                av_ps = psum.tile([P, H, DK], F32, tag="av", bufs=2)
+                for h in range(H):
+                    cols = slice(h * P, (h + 1) * P)
+                    nc.tensor.matmul_mx(
+                        out=av_ps[:, h, :],
+                        lhsT=e_codes[(b, n)][:, cols].bitcast(FP8X4), lhsT_scale=e_scales[(b, n)][:, cols],
+                        rhs=v_codes[(b, h)][:].bitcast(FP8X4), rhs_scale=v_scales[(b, h)][:],
+                        start=True, stop=True,
+                    )
+            else:
+                av_ps = psum.tile([P, H * NC, P], F32, tag="av", bufs=2)
+                for h in range(H):
+                    cols = slice(h * P, (h + 1) * P)
+                    for c in range(NC):
+                        chunk = slice(c * P, (c + 1) * P)
+                        nc.tensor.matmul_mx(
+                            out=av_ps[:, NC * h + c, :],
+                            lhsT=v_codes[(b, h)][:, chunk].bitcast(FP8X4), lhsT_scale=v_scales[(b, h)][:, chunk],
+                            rhs=e_codes[(b, n)][:, cols].bitcast(FP8X4), rhs_scale=e_scales[(b, n)][:, cols],
+                            start=True, stop=True,
+                        )
+            av[(b, n)] = av_ps
 
-        def group_rows(g, n):
-            r_g = units.tile([P, NB * P], BF16, tag="rows_grouped", align_bytes=64)
-            nc.vector.tensor_copy(
-                out=r_g[:].bitcast(F32).rearrange("p (j u) -> p j u", u=2), in_=rows_T[(g, n)][:].rearrange("p u j -> p j u")
-            )
-            rows_grouped[(g, n)] = r_g
+        def divide_transposed(b, n):
+            if b < FIRST_DIRECT:
+                r_g = blocks.tile([P, P, H, NC], BF16, tag="rows_grouped", align_bytes=64)
+                nc.vector.tensor_tensor(
+                    out=r_g[:], in0=av[(b, n)][:].rearrange("p (h c) j -> p j h c", h=H),
+                    in1=row_inv_bc[b][:, :, n, :].unsqueeze(3).to_broadcast([P, P, H, NC]), op=ALU.mult,
+                )
+                rows_grouped[(b, n)] = r_g[:].rearrange("p j h c -> p (j h c)")
 
-        def quantise_rows(g, n):
-            if g > 0 and n == 0:
-                a_c = heads.tile([P, S], U32, tag="a_codes", align_bytes=64)
-                a_s = heads.tile([P, S], U8, tag="a_scales", align_bytes=64)
-                a_codes[g], a_scales[g] = a_c, a_s
-            codes, scales = (wo_codes, wo_scales) if g == 0 else (a_codes[g], a_scales[g])
-            cols = slice(n * P, (n + 1) * P)
-            nc.vector.quantize_mx(
-                out=codes[:, cols].bitcast(FP8X4), scales=scales[:, cols],
-                in_=rows_grouped[(g, n)][:],
-            )
+        def divide_direct(b, n):
+            if b >= FIRST_DIRECT:
+                a_n = blocks.tile([P, D], BF16, tag="a_bf")
+                for h in range(H):
+                    nc.scalar.activation(
+                        out=a_n[:, h * DK : (h + 1) * DK], in_=av[(b, n)][:, h, :],
+                        func=ACT.Copy, scale=row_inv[(b, n)][:, h : h + 1],
+                    )
+                a_bf[(b, n)] = a_n
 
-        def project(g, n):
-            cols = slice(n * P, (n + 1) * P)
-            o_ps = psum_mx.tile([P, D], F32, tag="mx")
+        WO = B
+
+        def transpose_rows(b, n):
+            if b >= FIRST_DIRECT:
+                rows_ps = psum.tile([P, D // P, P], BF16, tag="av", bufs=2)
+                for t in range(D // P):
+                    feats = slice(t * P, (t + 1) * P)
+                    nc.tensor.transpose(
+                        out=rows_ps[:, t, :], in_=wo_sb[:, n, feats] if b == WO else a_bf[(b, n)][:, feats], identity=ident[:]
+                    )
+                rows_T[(b, n)] = rows_ps
+
+        def group_rows(b, n):
+            if b >= FIRST_DIRECT:
+                r_g = blocks.tile([P, P, H * NC], BF16, tag="rows_grouped", align_bytes=64, name="r_g")
+                nc.vector.tensor_copy(out=r_g[:], in_=rows_T[(b, n)][:].rearrange("p t j -> p j t"))
+                rows_grouped[(b, n)] = r_g[:].rearrange("p j t -> p (j t)")
+
+        def quantise_rows(b, n):
+            if b == WO:
+                cols = slice(n * P, (n + 1) * P)
+                codes, scales = wo_codes[:, cols], wo_scales[:, cols]
+            else:
+                a_c = blocks.tile([P, P], U32, tag="a_codes", align_bytes=64)
+                a_s = blocks.tile([P, P], U8, tag="a_scales", align_bytes=64)
+                a_codes[(b, n)], a_scales[(b, n)] = a_c, a_s
+                codes, scales = a_c[:], a_s[:]
+            nc.vector.quantize_mx(out=codes.bitcast(FP8X4), scales=scales, in_=rows_grouped[(b, n)])
+
+        def project(b, n):
+            o_ps = psum.tile([P, D], F32, tag="o", bufs=2)
             nc.tensor.matmul_mx(
                 out=o_ps[:],
-                lhsT=a_codes[g][:, cols].bitcast(FP8X4), lhsT_scale=a_scales[g][:, cols],
+                lhsT=a_codes[(b, n)][:].bitcast(FP8X4), lhsT_scale=a_scales[(b, n)][:],
                 rhs=wo_codes[:].bitcast(FP8X4), rhs_scale=wo_scales[:],
                 start=True, stop=True,
             )
-            proj[(g, n)] = o_ps
+            proj[(b, n)] = o_ps
 
-        def add_bias_and_store(g, n):
-            o_sb = units.tile([P, D], F32, tag="o_sb")
-            nc.vector.tensor_tensor(out=o_sb[:], in0=proj[(g, n)][:], in1=bias_bc[:], op=ALU.add)
-            nc.sync.dma_start(out=out[g - 1, n * P : (n + 1) * P, :], in_=o_sb[:])
+        def add_bias_and_store(b, n):
+            o_sb = blocks.tile([P, D], F32, tag="o_sb")
+            nc.vector.tensor_tensor(out=o_sb[:], in0=proj[(b, n)][:], in1=bias_bc[:], op=ALU.add)
+            nc.sync.dma_start(out=out[b, n * P : (n + 1) * P, :], in_=o_sb[:])
 
-        n_units = N_HEADS * NB
+        def load_ahead(b, n):
+            if n == 0 and b + 2 < B:
+                load_batch(b + 2)
 
-        def unit(step):
-            return divmod(step, NB) if 0 <= step < n_units else None
+        def exp1(b, n):
+            for h in range(H):
+                first_exp(b, n, h)
 
-        def rows_block(step):
-            g, n = divmod(step, H * NB)
-            return (g, n) if 0 <= g <= B and n < NB else None
+        def exp2(b, n):
+            for h in range(H):
+                second_exp(b, n, h)
 
-        DIVIDE_LAG = 8
-        ROWS_LAG = DIVIDE_LAG
+        def sc0(b, n):
+            negated_scores(b, n, 0)
 
-        for step in range(-2, n_units + ROWS_LAG + NB + 5):
-            u = unit(step + 2)
-            if u:
-                transpose_qk(*u)
-            u = unit(step + 1)
-            if u:
-                copy_qkT(*u)
-            u = unit(step - 2)
-            if u:
-                invert_window_sums(*u)
-            u = unit(step - 1)
-            if u:
-                first_exp(*u)
-            u = unit(step - 2)
-            if u:
-                second_exp(*u)
-            u = unit(step)
-            if u:
-                negated_scores(*u)
-                window_minima(*u)
-            u = unit(step - 3)
-            if u:
-                transpose_e(*u)
-            u = unit(step - 4)
-            if u:
-                group_e(*u)
-            u = unit(step - 5)
-            if u:
-                quantise_e(*u)
+        def sc1(b, n):
+            negated_scores(b, n, 1)
 
-            u = unit(step)
-            if u and u[1] == 2:
-                group_v(u[0])
-            if u and u[1] == 3:
-                quantise_v(u[0])
-            u = unit(step - 3)
-            if u and u[1] == NB - 1:
-                invert_row_sums(u[0])
-            u = unit(step - 6)
-            if u and u[1] == NB - 1:
-                e_times_v(u[0])
-            u = unit(step - 7)
-            if u and u[1] == NB - 1:
-                divide_by_row_sums(u[0])
+        def min0(b, n):
+            window_minima(b, n, 0)
 
-            r = rows_block(step - ROWS_LAG)
-            if r:
-                transpose_rows(*r)
-            r = rows_block(step - ROWS_LAG - 1)
-            if r:
-                group_rows(*r)
-            r = rows_block(step - ROWS_LAG - 2)
-            if r:
-                quantise_rows(*r)
-            r = rows_block(step - ROWS_LAG - 3)
-            if r and r[0] > 0:
-                project(*r)
-            r = rows_block(step - ROWS_LAG - 4)
-            if r and r[0] > 0:
-                add_bias_and_store(*r)
+        def min1(b, n):
+            window_minima(b, n, 1)
+
+        def vgroup(b, n):
+            if n in (0, 1):
+                group_v(b, n)
+
+        def vquant(b, n):
+            if n in (0, 1):
+                quantise_v(b, n)
+
+        def wo_t(b, n):
+            if b == 0:
+                transpose_rows(WO, n)
+
+        def wo_g(b, n):
+            if b == 0:
+                group_rows(WO, n)
+
+        def wo_q(b, n):
+            if b == 0:
+                quantise_rows(WO, n)
+
+        order = [(b, n) for b in range(B) for n in range(NB)]
+        stages = [
+            (load_ahead, 0, 0),
+            (transpose_e, 2, 2),
+            (transpose_qk, -2, -2),
+            (transpose_rows, 99, 5),
+            (wo_t, 2, 2),
+            (exp1, 0, 0),
+            (exp2, 1, 1),
+            (invert_row_sums, 2, 2),
+            (quantise_e, 3, 3),
+            (divide_transposed, 8, 99),
+            (add_bias_and_store, 10, 8),
+            (invert_window_sums, 0, 0),
+            (sc0, -1, -1),
+            (min0, -1, -1),
+            (sc1, -1, -1),
+            (min1, -1, -1),
+            (group_e, 2, 2),
+            (copy_qkT, -2, -2),
+            (divide_direct, 99, 4),
+            (vgroup, 0, 0),
+            (vquant, 1, 1),
+            (wo_g, 2, 2),
+            (wo_q, 3, 3),
+            (group_rows, 99, 5),
+            (quantise_rows, 8, 6),
+            (e_times_v, 7, 3),
+            (project, 9, 7),
+        ]
+        steps = range(-3, len(order) + 14)
+        with tc.manual_schedule():
+            for step in steps:
+                for stage, lag, lag_direct in stages:
+                    for b, n in order:
+                        if step - (lag_direct if b >= FIRST_DIRECT else lag) == b * NB + n:
+                            stage(b, n)

@@ -354,33 +354,33 @@ def tile_multiheadattention_pa_t_kernel(tc, q, k, v, Wo_w, Wo_b, out):
 
         order = [(b, n) for b in range(B) for n in range(NB)]
         stages = [
-            (load_ahead, 0, 0),
             (transpose_e, 2, 2),
-            (transpose_qk, -2, -2),
-            (transpose_rows, 99, 5),
-            (wo_t, 2, 2),
+            (divide_direct, 99, 4),
+            (invert_window_sums, 1, 1),
             (exp1, 0, 0),
-            (exp2, 1, 1),
-            (invert_row_sums, 2, 2),
+            (add_bias_and_store, 10, 8),
             (quantise_e, 3, 3),
             (divide_transposed, 8, 99),
-            (add_bias_and_store, 10, 8),
-            (invert_window_sums, 0, 0),
-            (sc0, -1, -1),
-            (min0, -1, -1),
-            (sc1, -1, -1),
-            (min1, -1, -1),
+            (transpose_qk, -2, -2),
+            (transpose_rows, 99, 5),
+            (wo_t, 4, 4),
+            (quantise_rows, 9, 6),
+            (wo_q, 6, 6),
             (group_e, 2, 2),
-            (copy_qkT, -2, -2),
-            (divide_direct, 99, 4),
-            (vgroup, 0, 0),
-            (vquant, 1, 1),
-            (wo_g, 2, 2),
-            (wo_q, 3, 3),
-            (group_rows, 99, 5),
-            (quantise_rows, 8, 6),
-            (e_times_v, 7, 3),
+            (exp2, 1, 1),
+            (sc0, -1, -1),
+            (sc1, -1, -1),
+            (invert_row_sums, 2, 2),
             (project, 9, 7),
+            (e_times_v, 7, 3),
+            (group_rows, 99, 5),
+            (wo_g, 5, 5),
+            (vquant, 1, 1),
+            (vgroup, 0, 0),
+            (load_ahead, 2, 2),
+            (min0, -1, -1),
+            (copy_qkT, -2, -2),
+            (min1, -1, -1),
         ]
         steps = range(-3, len(order) + 14)
         with tc.manual_schedule():

@@ -19,7 +19,7 @@ NB = S // P
 NC = DK // P
 N_HEADS = B * H
 FIRST_DIRECT = 6
-E_BUFS = 8
+E_BUFS = 12
 MASKED = 1.0e30
 
 FLOPS = 2 * B * H * S * S * DK * 2 + 2 * B * S * D * D
@@ -358,21 +358,21 @@ def tile_multiheadattention_pa_t_kernel(tc, q, k, v, Wo_w, Wo_b, out):
             (divide_direct, 99, 4),
             (invert_window_sums, 1, 1),
             (exp1, 0, 0),
-            (add_bias_and_store, 10, 8),
+            (add_bias_and_store, 12, 8),
             (quantise_e, 3, 3),
-            (divide_transposed, 8, 99),
+            (divide_transposed, 10, 99),
             (transpose_qk, -2, -2),
             (transpose_rows, 99, 5),
             (wo_t, 4, 4),
-            (quantise_rows, 9, 6),
+            (quantise_rows, 11, 6),
             (wo_q, 6, 6),
             (group_e, 2, 2),
             (exp2, 1, 1),
             (sc0, -1, -1),
             (sc1, -1, -1),
             (invert_row_sums, 2, 2),
-            (project, 9, 7),
-            (e_times_v, 7, 3),
+            (project, 11, 7),
+            (e_times_v, 9, 3),
             (group_rows, 99, 5),
             (wo_g, 5, 5),
             (vquant, 1, 1),

@@ -29,9 +29,9 @@ def tile_multiheadattention_pa_t_kernel(tc, q, k, v, Wo_w, Wo_b, out):
     nc = tc.nc
     with ExitStack() as ctx:
         const = ctx.enter_context(tc.tile_pool(name="const", bufs=1))
-        inputs = ctx.enter_context(tc.tile_pool(name="inputs", bufs=B))
-        batches = ctx.enter_context(tc.tile_pool(name="batches", bufs=3))
-        blocks = ctx.enter_context(tc.tile_pool(name="blocks", bufs=3))
+        inputs = ctx.enter_context(tc.tile_pool(name="inputs", bufs=4))
+        batches = ctx.enter_context(tc.tile_pool(name="batches", bufs=5))
+        blocks = ctx.enter_context(tc.tile_pool(name="blocks", bufs=4))
         e_pool = ctx.enter_context(tc.tile_pool(name="e_pool", bufs=E_BUFS))
         stats = ctx.enter_context(tc.tile_pool(name="stats", bufs=8))
         psum = ctx.enter_context(tc.psum_pool(name="psum", bufs=1))
@@ -41,30 +41,39 @@ def tile_multiheadattention_pa_t_kernel(tc, q, k, v, Wo_w, Wo_b, out):
         wo_sb = const.tile([P, NB, D], BF16)
         bias_bc = const.tile([P, D], BF16)
 
-        def load_batch(b):
-            q_b = inputs.tile([P, H, NB, DK], BF16)
-            k_b = inputs.tile([P, H, NB, DK], BF16)
-            v_b = inputs.tile([P, H, NB, DK], BF16)
-            if b == 0:
-                for n in range(NB):
-                    rows = slice(n * P, (n + 1) * P)
-                    nc.sync.dma_start(out=q_b[:, :, n], in_=q[b, :, rows, :].rearrange("h p d -> p h d"))
-                    nc.sync.dma_start(out=k_b[:, :, n], in_=k[b, :, rows, :].rearrange("h p d -> p h d"))
-            else:
-                nc.sync.dma_start(out=q_b[:].rearrange("p h n d -> p (h n) d"), in_=q[b].rearrange("h (n p) d -> p (h n) d", p=P))
-                nc.sync.dma_start(out=k_b[:].rearrange("p h n d -> p (h n) d"), in_=k[b].rearrange("h (n p) d -> p (h n) d", p=P))
+        def load_qk_block(b, n):
+            if n == 0:
+                q_sb.append(inputs.tile([P, H, NB, DK], BF16, name="q_b"))
+                k_sb.append(inputs.tile([P, H, NB, DK], BF16, name="k_b"))
+            rows = slice(n * P, (n + 1) * P)
+            nc.sync.dma_start(out=q_sb[b][:, :, n], in_=q[b, :, rows, :].rearrange("h p d -> p h d"))
+            nc.sync.dma_start(out=k_sb[b][:, :, n], in_=k[b, :, rows, :].rearrange("h p d -> p h d"))
+
+        def load_qk(b):
+            q_sb.append(inputs.tile([P, H, NB, DK], BF16, name="q_b"))
+            k_sb.append(inputs.tile([P, H, NB, DK], BF16, name="k_b"))
+            nc.sync.dma_start(out=q_sb[b][:].rearrange("p h n d -> p (h n) d"), in_=q[b].rearrange("h (n p) d -> p (h n) d", p=P))
+            nc.sync.dma_start(out=k_sb[b][:].rearrange("p h n d -> p (h n) d"), in_=k[b].rearrange("h (n p) d -> p (h n) d", p=P))
+
+        def load_v(b):
+            v_sb.append(inputs.tile([P, H, NB, DK], BF16, name="v_b"))
             nc.sync.dma_start(
-                out=v_b[:].rearrange("p h (u c) d -> p h u c d", u=2),
+                out=v_sb[b][:].rearrange("p h (u c) d -> p h u c d", u=2),
                 in_=v[b].rearrange("h (u p c) d -> p h u c d", u=2, c=2),
             )
-            q_sb.append(q_b)
-            k_sb.append(k_b)
-            v_sb.append(v_b)
 
-        load_batch(0)
+        def load_batch(b):
+            load_qk(b)
+            load_v(b)
+
+        for n in range(NB):
+            load_qk_block(0, n)
+            if n == 2:
+                load_v(0)
+        load_qk(1)
         nc.sync.dma_start(out=wo_sb[:], in_=Wo_w.rearrange("(n p) f -> p n f", p=P))
+        load_v(1)
         nc.sync.dma_start(out=bias_bc[:], in_=Wo_b.partition_broadcast(P))
-        load_batch(1)
 
         neg_ident = const.tile([P, P], BF16)
         nc.gpsimd.memset(neg_ident[:], 0.0)
@@ -121,7 +130,7 @@ def tile_multiheadattention_pa_t_kernel(tc, q, k, v, Wo_w, Wo_b, out):
             v_codes[(b, h)], v_scales[(b, h)] = v_c, v_s
 
         def transpose_qk(b, n):
-            qk_ps = psum.tile([P, H, 2, NC, P], BF16, tag="qk")
+            qk_ps = psum.tile([P, H, 2, NC, P], BF16, tag="e" if b == 0 and n % 2 else "qk")
             for h in range(H):
                 for c in range(NC):
                     chunk = slice(c * P, (c + 1) * P)
@@ -129,28 +138,50 @@ def tile_multiheadattention_pa_t_kernel(tc, q, k, v, Wo_w, Wo_b, out):
                     nc.tensor.transpose(out=qk_ps[:, h, 1, c, :], in_=k_sb[b][:, h, n, chunk], identity=ident[:])
             qkT_psum[(b, n)] = qk_ps
 
-        def copy_qkT(b, n):
+        def copy_s(b, n):
+            if not (n in (1,) or (b == 0 and n % 2)):
+                copy_any(b, n, nc.scalar.copy)
+
+        def copy_v(b, n):
+            if n in (1,) or (b == 0 and n % 2):
+                copy_any(b, n, nc.vector.tensor_copy)
+
+        def copy_any(b, n, copy):
             if n == 0:
                 qkT_b = batches.tile([P, NB, H, 2, NC, P], BF16, tag="qkT")
                 qkT[b] = qkT_b
-            (nc.vector.tensor_copy if n in (1,) else nc.scalar.copy)(out=qkT[b][:, n], in_=qkT_psum[(b, n)][:])
+            copy(out=qkT[b][:, n], in_=qkT_psum[(b, n)][:])
 
         def negated_scores(b, n, h):
             keys = (n + 1) * P
-            sc = psum_sc.tile([P, S], F32, tag="sc")
-            by_window = sc[:, :keys].rearrange("p (w j) -> p w j", j=P)
-            nc.tensor.matmul(out=by_window, lhsT=qkT[b][:, n, h, 0, 0, :], rhs=qkT[b][:, : n + 1, h, 1, 0, :], start=True, stop=False)
-            nc.tensor.matmul(out=sc[:, n * P : keys], lhsT=ident[:], rhs=mask[:], start=False, stop=False)
-            nc.tensor.matmul(out=by_window, lhsT=qkT[b][:, n, h, 0, 1, :], rhs=qkT[b][:, : n + 1, h, 1, 1, :], start=False, stop=True)
-            scores[(b, n, h)] = sc
+            if n < 2:
+                if h == 1:
+                    return
+                sc = psum_sc.tile([P, H, (n + 1) * P], F32, tag="sc")
+                parts = [(h2, sc[:, h2]) for h2 in range(H)]
+            else:
+                sc = psum_sc.tile([P, S], F32, tag="sc", name="sc")
+                parts = [(h, sc[:, :keys])]
+            for h2, out_ps in parts:
+                by_window = out_ps.rearrange("p (w j) -> p w j", j=P)
+                nc.tensor.matmul(out=by_window, lhsT=qkT[b][:, n, h2, 0, 0, :], rhs=qkT[b][:, : n + 1, h2, 1, 0, :], start=True, stop=False)
+                nc.tensor.matmul(out=out_ps[:, n * P : keys], lhsT=ident[:], rhs=mask[:], start=False, stop=False)
+                nc.tensor.matmul(out=by_window, lhsT=qkT[b][:, n, h2, 0, 1, :], rhs=qkT[b][:, : n + 1, h2, 1, 1, :], start=False, stop=True)
+                scores[(b, n, h2)] = out_ps
+            if n < 2:
+                scores[(b, n)] = sc[:].rearrange("p h (w j) -> p h w j", j=P)
+            else:
+                scores[(b, n, h, "w")] = by_window
 
         def window_minima(b, n, h):
-            sh = stats.tile([P, NB], F32, tag="shift")
-            nc.vector.tensor_reduce(
-                out=sh[:, : n + 1], in_=scores[(b, n, h)][:, : (n + 1) * P].rearrange("p (w j) -> p w j", j=P),
-                axis=AXIS_X, op=ALU.min,
-            )
-            shift[(b, n, h)] = sh
+            if h == 0:
+                sh = stats.tile([P, H, NB], F32, tag="shift")
+                shift[(b, n)] = sh
+            if n < 2:
+                if h == 0:
+                    nc.vector.tensor_reduce(out=shift[(b, n)][:, :, : n + 1], in_=scores[(b, n)], axis=AXIS_X, op=ALU.min)
+            else:
+                nc.vector.tensor_reduce(out=shift[(b, n)][:, h, : n + 1], in_=scores[(b, n, h, "w")], axis=AXIS_X, op=ALU.min)
 
         def first_exp(b, n, h):
             if h == 0:
@@ -160,7 +191,7 @@ def tile_multiheadattention_pa_t_kernel(tc, q, k, v, Wo_w, Wo_b, out):
             for w in range(n + 1):
                 nc.scalar.activation(
                     out=ex[(b, n)][:, h, w, :], in_=scores[(b, n, h)][:, w * P : (w + 1) * P], func=ACT.Exp,
-                    scale=-1.0, bias=shift[(b, n, h)][:, w : w + 1], accum_out=win_sum[(b, n)][:, h, w : w + 1],
+                    scale=-1.0, bias=shift[(b, n)][:, h, w : w + 1], accum_out=win_sum[(b, n)][:, h, w : w + 1],
                 )
 
         def invert_window_sums(b, n):
@@ -222,7 +253,7 @@ def tile_multiheadattention_pa_t_kernel(tc, q, k, v, Wo_w, Wo_b, out):
 
         def e_times_v(b, n):
             if b >= FIRST_DIRECT:
-                av_ps = psum.tile([P, H, DK], F32, tag="av", bufs=2)
+                av_ps = psum.tile([P, H, DK], F32, tag="mx", bufs=4)
                 for h in range(H):
                     cols = slice(h * P, (h + 1) * P)
                     nc.tensor.matmul_mx(
@@ -232,7 +263,7 @@ def tile_multiheadattention_pa_t_kernel(tc, q, k, v, Wo_w, Wo_b, out):
                         start=True, stop=True,
                     )
             else:
-                av_ps = psum.tile([P, H * NC, P], F32, tag="av", bufs=2)
+                av_ps = psum.tile([P, H * NC, P], F32, tag="mx", bufs=4)
                 for h in range(H):
                     cols = slice(h * P, (h + 1) * P)
                     for c in range(NC):
@@ -268,7 +299,7 @@ def tile_multiheadattention_pa_t_kernel(tc, q, k, v, Wo_w, Wo_b, out):
 
         def transpose_rows(b, n):
             if b >= FIRST_DIRECT:
-                rows_ps = psum.tile([P, D // P, P], BF16, tag="av", bufs=2)
+                rows_ps = psum.tile([P, D // P, P], BF16, tag="mx", bufs=4)
                 for t in range(D // P):
                     feats = slice(t * P, (t + 1) * P)
                     nc.tensor.transpose(
@@ -294,7 +325,7 @@ def tile_multiheadattention_pa_t_kernel(tc, q, k, v, Wo_w, Wo_b, out):
             nc.vector.quantize_mx(out=codes.bitcast(FP8X4), scales=scales, in_=rows_grouped[(b, n)])
 
         def project(b, n):
-            o_ps = psum.tile([P, D], F32, tag="o", bufs=2)
+            o_ps = psum.tile([P, D], F32, tag="mx", bufs=4)
             nc.tensor.matmul_mx(
                 out=o_ps[:],
                 lhsT=a_codes[(b, n)][:].bitcast(FP8X4), lhsT_scale=a_scales[(b, n)][:],
@@ -355,32 +386,34 @@ def tile_multiheadattention_pa_t_kernel(tc, q, k, v, Wo_w, Wo_b, out):
         order = [(b, n) for b in range(B) for n in range(NB)]
         stages = [
             (transpose_e, 2, 2),
-            (divide_direct, 99, 4),
-            (invert_window_sums, 1, 1),
-            (exp1, 0, 0),
-            (add_bias_and_store, 12, 8),
-            (quantise_e, 3, 3),
-            (divide_transposed, 10, 99),
+            (add_bias_and_store, 11, 8),
             (transpose_qk, -2, -2),
+            (divide_transposed, 9, 99),
             (transpose_rows, 99, 5),
             (wo_t, 4, 4),
-            (quantise_rows, 11, 6),
-            (wo_q, 6, 6),
-            (group_e, 2, 2),
-            (exp2, 1, 1),
+            (quantise_rows, 10, 99),
             (sc0, -1, -1),
             (sc1, -1, -1),
+            (exp1, 0, 0),
+            (divide_direct, 99, 4),
+            (invert_window_sums, 1, 1),
+            (group_e, 2, 2),
+            (exp2, 1, 1),
+            (vgroup, 0, 0),
+            (copy_v, -2, -2),
+            (copy_s, -2, -2),
+            (vquant, 2, 1),
+            (quantise_rows, 99, 6),
+            (quantise_e, 3, 3),
+            (wo_q, 7, 7),
             (invert_row_sums, 2, 2),
-            (project, 11, 7),
-            (e_times_v, 9, 3),
             (group_rows, 99, 5),
             (wo_g, 5, 5),
-            (vquant, 1, 1),
-            (vgroup, 0, 0),
-            (load_ahead, 2, 2),
+            (load_ahead, 0, 0),
             (min0, -1, -1),
-            (copy_qkT, -2, -2),
             (min1, -1, -1),
+            (project, 10, 7),
+            (e_times_v, 8, 3),
         ]
         steps = range(-3, len(order) + 14)
         with tc.manual_schedule():

@@ -18,7 +18,8 @@ P = 128
 NB = S // P
 NC = DK // P
 N_HEADS = B * H
-FIRST_DIRECT = 6
+FIRST_DIRECT = 7
+COPIES = 4
 E_BUFS = 12
 MASKED = 1.0e30
 
@@ -30,8 +31,9 @@ def tile_multiheadattention_pa_t_kernel(tc, q, k, v, Wo_w, Wo_b, out):
     with ExitStack() as ctx:
         const = ctx.enter_context(tc.tile_pool(name="const", bufs=1))
         inputs = ctx.enter_context(tc.tile_pool(name="inputs", bufs=4))
-        batches = ctx.enter_context(tc.tile_pool(name="batches", bufs=5))
+        batches = ctx.enter_context(tc.tile_pool(name="batches", bufs=4))
         blocks = ctx.enter_context(tc.tile_pool(name="blocks", bufs=4))
+        outs = ctx.enter_context(tc.tile_pool(name="outs", bufs=8))
         e_pool = ctx.enter_context(tc.tile_pool(name="e_pool", bufs=E_BUFS))
         stats = ctx.enter_context(tc.tile_pool(name="stats", bufs=8))
         psum = ctx.enter_context(tc.psum_pool(name="psum", bufs=1))
@@ -70,7 +72,8 @@ def tile_multiheadattention_pa_t_kernel(tc, q, k, v, Wo_w, Wo_b, out):
             load_qk_block(0, n)
             if n == 2:
                 load_v(0)
-        load_qk(1)
+        for n in range(NB):
+            load_qk_block(1, n)
         nc.sync.dma_start(out=wo_sb[:], in_=Wo_w.rearrange("(n p) f -> p n f", p=P))
         load_v(1)
         nc.sync.dma_start(out=bias_bc[:], in_=Wo_b.partition_broadcast(P))
@@ -109,7 +112,7 @@ def tile_multiheadattention_pa_t_kernel(tc, q, k, v, Wo_w, Wo_b, out):
         wo_scales = const.tile([P, D], U8, align_bytes=64)
 
         qkT_psum, qkT, v_grouped, v_codes, v_scales, row_inv, av = {}, {}, {}, {}, {}, {}, {}
-        row_inv_bc, avT = {}, {}
+        row_inv_bc, row_sums = {}, {}
         scores, shift, win_sum, win_inv, ex, eT, e_grouped, e_codes, e_scales = {}, {}, {}, {}, {}, {}, {}, {}, {}
         a_bf, rows_T, rows_grouped, a_codes, a_scales, proj = {}, {}, {}, {}, {}, {}
 
@@ -139,11 +142,11 @@ def tile_multiheadattention_pa_t_kernel(tc, q, k, v, Wo_w, Wo_b, out):
             qkT_psum[(b, n)] = qk_ps
 
         def copy_s(b, n):
-            if not (n in (1,) or (b == 0 and n % 2)):
+            if not (n % 2 and b < 2 or n == 1):
                 copy_any(b, n, nc.scalar.copy)
 
         def copy_v(b, n):
-            if n in (1,) or (b == 0 and n % 2):
+            if n % 2 and b < 2 or n == 1:
                 copy_any(b, n, nc.vector.tensor_copy)
 
         def copy_any(b, n, copy):
@@ -206,24 +209,39 @@ def tile_multiheadattention_pa_t_kernel(tc, q, k, v, Wo_w, Wo_b, out):
                     scale=win_inv[(b, n)][:, h, w : w + 1], accum_out=e_sums[b % 2][:, n, h, w : w + 1],
                 )
 
-        def invert_row_sums(b, n):
+        def sum_rows(b, n):
             if b >= FIRST_DIRECT:
                 row_sum = stats.tile([P, H], F32, tag="row_sum")
                 nc.vector.tensor_reduce(out=row_sum[:], in_=e_sums[b % 2][:, n], axis=AXIS_X, op=ALU.add)
-                row_inv_n = stats.tile([P, H], F32, tag="row_inv")
-                nc.vector.reciprocal(out=row_inv_n[:], in_=row_sum[:])
-                row_inv[(b, n)] = row_inv_n
+                row_sums[(b, n)] = row_sum
             elif n == NB - 1:
                 row_sum_b = stats.tile([P, NB, H], F32, tag="row_sum_b")
                 nc.vector.tensor_reduce(out=row_sum_b[:], in_=e_sums[b % 2][:], axis=AXIS_X, op=ALU.add)
+                row_sums[b] = row_sum_b
+
+        def parked_rows(b, c):
+            first = (NB - 1) * P + c * P // COPIES
+            return out[b, first : first + 2, :]
+
+        def invert_row_sums(b, n):
+            if b >= FIRST_DIRECT:
+                row_inv_n = stats.tile([P, H], F32, tag="row_inv")
+                nc.vector.reciprocal(out=row_inv_n[:], in_=row_sums[(b, n)][:])
+                row_inv[(b, n)] = row_inv_n
+            elif n == NB - 1:
                 row_inv_b = stats.tile([P, NB, H], F32, tag="row_inv_b")
-                nc.vector.reciprocal(out=row_inv_b[:], in_=row_sum_b[:])
-                parked = out[b, S - 2 : S, :]
-                nc.sync.dma_start(out=parked.rearrange("r (p x) -> (r p) x", x=NB * H), in_=row_inv_b[:].rearrange("p n h -> p (n h)"))
+                nc.vector.reciprocal(out=row_inv_b[:], in_=row_sums[b][:])
                 bc = batches.tile([P, P, NB, H], F32, tag="row_inv_bc")
-                nc.sync.dma_start(
-                    out=bc[:].rearrange("p j n h -> p (j n h)"), in_=parked.rearrange("r f -> (r f)").partition_broadcast(P)
-                )
+                for c in range(COPIES):
+                    nc.sync.dma_start(
+                        out=parked_rows(b, c).rearrange("r (p x) -> (r p) x", x=NB * H), in_=row_inv_b[:].rearrange("p n h -> p (n h)")
+                    )
+                for c in range(COPIES):
+                    readers = slice(c * P // COPIES, (c + 1) * P // COPIES)
+                    nc.sync.dma_start(
+                        out=bc[readers].rearrange("p j n h -> p (j n h)"),
+                        in_=parked_rows(b, c).rearrange("r f -> (r f)").partition_broadcast(P // COPIES),
+                    )
                 row_inv_bc[b] = bc
 
         def transpose_words(out_ps, rows):
@@ -310,7 +328,7 @@ def tile_multiheadattention_pa_t_kernel(tc, q, k, v, Wo_w, Wo_b, out):
         def group_rows(b, n):
             if b >= FIRST_DIRECT:
                 r_g = blocks.tile([P, P, H * NC], BF16, tag="rows_grouped", align_bytes=64, name="r_g")
-                nc.vector.tensor_copy(out=r_g[:], in_=rows_T[(b, n)][:].rearrange("p t j -> p j t"))
+                (nc.scalar.copy if b < B else nc.vector.tensor_copy)(out=r_g[:], in_=rows_T[(b, n)][:].rearrange("p t j -> p j t"))
                 rows_grouped[(b, n)] = r_g[:].rearrange("p j t -> p (j t)")
 
         def quantise_rows(b, n):
@@ -335,7 +353,7 @@ def tile_multiheadattention_pa_t_kernel(tc, q, k, v, Wo_w, Wo_b, out):
             proj[(b, n)] = o_ps
 
         def add_bias_and_store(b, n):
-            o_sb = blocks.tile([P, D], F32, tag="o_sb")
+            o_sb = outs.tile([P, D], F32, tag="o_sb")
             nc.vector.tensor_tensor(out=o_sb[:], in0=proj[(b, n)][:], in1=bias_bc[:], op=ALU.add)
             nc.sync.dma_start(out=out[b, n * P : (n + 1) * P, :], in_=o_sb[:])
 
@@ -385,35 +403,39 @@ def tile_multiheadattention_pa_t_kernel(tc, q, k, v, Wo_w, Wo_b, out):
 
         order = [(b, n) for b in range(B) for n in range(NB)]
         stages = [
-            (transpose_e, 2, 2),
-            (add_bias_and_store, 11, 8),
-            (transpose_qk, -2, -2),
-            (divide_transposed, 9, 99),
-            (transpose_rows, 99, 5),
-            (wo_t, 4, 4),
-            (quantise_rows, 10, 99),
-            (sc0, -1, -1),
-            (sc1, -1, -1),
-            (exp1, 0, 0),
-            (divide_direct, 99, 4),
             (invert_window_sums, 1, 1),
-            (group_e, 2, 2),
-            (exp2, 1, 1),
-            (vgroup, 0, 0),
+            (transpose_qk, -2, -2),
+            (load_ahead, -1, -1),
+            (vgroup, 1, 1),
+            (divide_transposed, 8, 99),
+            (add_bias_and_store, 9, 99),
+            (transpose_rows, 99, 6),
+            (wo_t, 2, 2),
+            (sc0, -1, -1),
+            (quantise_rows, 8, 7),
             (copy_v, -2, -2),
+            (transpose_e, 2, 2),
+            (sc1, -1, -1),
+            (sum_rows, 2, 2),
+            (add_bias_and_store, 99, 8),
+            (e_times_v, 7, 99),
+            (exp1, 0, 0),
+            (project, 8, 99),
+            (vquant, 4, 3),
+            (invert_row_sums, 2, 3),
             (copy_s, -2, -2),
-            (vquant, 2, 1),
-            (quantise_rows, 99, 6),
-            (quantise_e, 3, 3),
-            (wo_q, 7, 7),
-            (invert_row_sums, 2, 2),
-            (group_rows, 99, 5),
-            (wo_g, 5, 5),
-            (load_ahead, 0, 0),
             (min0, -1, -1),
+            (wo_g, 3, 3),
+            (quantise_e, 4, 99),
+            (divide_direct, 99, 5),
+            (project, 99, 7),
+            (e_times_v, 99, 4),
+            (group_rows, 99, 6),
+            (exp2, 1, 1),
+            (quantise_e, 99, 3),
             (min1, -1, -1),
-            (project, 10, 7),
-            (e_times_v, 8, 3),
+            (wo_q, 4, 4),
+            (group_e, 2, 2),
         ]
         steps = range(-3, len(order) + 14)
         with tc.manual_schedule():

from contextlib import ExitStack

import concourse.mybir as mybir
from concourse.masks import make_identity

BF16 = mybir.dt.bfloat16
F32 = mybir.dt.float32
U32 = mybir.dt.uint32
U8 = mybir.dt.uint8
FP8X4 = mybir.dt.float8_e4m3fn_x4
ALU = mybir.AluOpType
ACT = mybir.ActivationFunctionType
AXIS_X = mybir.AxisListType.X

B, H, S, DK = 8, 2, 512, 256
D = H * DK
P = 128
NB = S // P
NC = DK // P
N_HEADS = B * H
FIRST_DIRECT = 7
COPIES = 4
E_BUFS = 12
MASKED = 1.0e30

FLOPS = 2 * B * H * S * S * DK * 2 + 2 * B * S * D * D


def tile_multiheadattention_pa_t_kernel(tc, q, k, v, Wo_w, Wo_b, out):
    nc = tc.nc
    with ExitStack() as ctx:
        const = ctx.enter_context(tc.tile_pool(name="const", bufs=1))
        inputs = ctx.enter_context(tc.tile_pool(name="inputs", bufs=4))
        batches = ctx.enter_context(tc.tile_pool(name="batches", bufs=4))
        blocks = ctx.enter_context(tc.tile_pool(name="blocks", bufs=4))
        outs = ctx.enter_context(tc.tile_pool(name="outs", bufs=8))
        e_pool = ctx.enter_context(tc.tile_pool(name="e_pool", bufs=E_BUFS))
        stats = ctx.enter_context(tc.tile_pool(name="stats", bufs=8))
        psum = ctx.enter_context(tc.psum_pool(name="psum", bufs=1))
        psum_sc = ctx.enter_context(tc.psum_pool(name="psum_sc", bufs=2))

        q_sb, k_sb, v_sb = [], [], []
        wo_sb = const.tile([P, NB, D], BF16)
        bias_bc = const.tile([P, D], BF16)

        def load_qk_block(b, n):
            if n == 0:
                q_sb.append(inputs.tile([P, H, NB, DK], BF16, name="q_b"))
                k_sb.append(inputs.tile([P, H, NB, DK], BF16, name="k_b"))
            rows = slice(n * P, (n + 1) * P)
            nc.sync.dma_start(out=q_sb[b][:, :, n], in_=q[b, :, rows, :].rearrange("h p d -> p h d"))
            nc.sync.dma_start(out=k_sb[b][:, :, n], in_=k[b, :, rows, :].rearrange("h p d -> p h d"))

        def load_qk(b):
            q_sb.append(inputs.tile([P, H, NB, DK], BF16, name="q_b"))
            k_sb.append(inputs.tile([P, H, NB, DK], BF16, name="k_b"))
            nc.sync.dma_start(out=q_sb[b][:].rearrange("p h n d -> p (h n) d"), in_=q[b].rearrange("h (n p) d -> p (h n) d", p=P))
            nc.sync.dma_start(out=k_sb[b][:].rearrange("p h n d -> p (h n) d"), in_=k[b].rearrange("h (n p) d -> p (h n) d", p=P))

        def load_v(b):
            v_sb.append(inputs.tile([P, H, NB, DK], BF16, name="v_b"))
            nc.sync.dma_start(
                out=v_sb[b][:].rearrange("p h (u c) d -> p h u c d", u=2),
                in_=v[b].rearrange("h (u p c) d -> p h u c d", u=2, c=2),
            )

        def load_batch(b):
            load_qk(b)
            load_v(b)

        for n in range(NB):
            load_qk_block(0, n)
            if n == 2:
                load_v(0)
        for n in range(NB):
            load_qk_block(1, n)
        nc.sync.dma_start(out=wo_sb[:], in_=Wo_w.rearrange("(n p) f -> p n f", p=P))
        load_v(1)
        nc.sync.dma_start(out=bias_bc[:], in_=Wo_b.partition_broadcast(P))

        neg_ident = const.tile([P, P], BF16)
        nc.gpsimd.memset(neg_ident[:], 0.0)
        nc.gpsimd.affine_select(
            out=neg_ident[:], in_=neg_ident[:], pattern=[[-1, P]], compare_op=ALU.not_equal,
            fill=-1.0 / 16.0, base=0, channel_multiplier=1,
        )
        ident = const.tile([P, P], BF16)
        make_identity(nc, ident[:])
        mask_f32 = const.tile([P, P], F32)
        nc.gpsimd.memset(mask_f32[:], 0.0)
        nc.gpsimd.affine_select(
            out=mask_f32[:], in_=mask_f32[:], pattern=[[-1, P]], compare_op=ALU.is_ge,
            fill=MASKED, base=0, channel_multiplier=1,
        )
        mask = const.tile([P, P], BF16)
        nc.vector.tensor_copy(out=mask[:], in_=mask_f32[:])
        ident_f32 = const.tile([P, P], F32)
        make_identity(nc, ident_f32[:])

        e_bf, e_sums = [], []
        for n in range(NB):
            e_bf_n = const.tile([P, H, NB, P], BF16, name="e_bf_%d" % n)
            if n < NB - 1:
                nc.vector.memset(e_bf_n[:, :, n + 1 :, :], 1.0)
            e_bf.append(e_bf_n)
        for parity in range(2):
            e_sums_x = const.tile([P, NB, H, NB], F32, name="e_sums_%d" % parity)
            nc.vector.memset(e_sums_x[:], float(P))
            e_sums.append(e_sums_x)

        wo_codes = const.tile([P, D], U32, align_bytes=64)
        wo_scales = const.tile([P, D], U8, align_bytes=64)

        qkT_psum, qkT, v_grouped, v_codes, v_scales, row_inv, av = {}, {}, {}, {}, {}, {}, {}
        row_inv_bc, row_sums = {}, {}
        scores, shift, win_sum, win_inv, ex, eT, e_grouped, e_codes, e_scales = {}, {}, {}, {}, {}, {}, {}, {}, {}
        a_bf, rows_T, rows_grouped, a_codes, a_scales, proj = {}, {}, {}, {}, {}, {}

        def group_v(b, h):
            v_g = batches.tile([P, DK, NB], BF16, tag="v_grouped", align_bytes=64)
            nc.vector.tensor_copy(
                out=v_g[:].rearrange("p (d r) t -> p d t r", r=4),
                in_=v_sb[b][:, h].rearrange("p t (d r) -> p d t r", r=4),
            )
            v_grouped[(b, h)] = v_g

        def quantise_v(b, h):
            v_c = batches.tile([P, DK], U32, tag="v_codes_%d" % h, align_bytes=64, name="v_c")
            v_s = batches.tile([P, DK], U8, tag="v_scales_%d" % h, align_bytes=64, name="v_s")
            nc.vector.quantize_mx(
                out=v_c[:].bitcast(FP8X4), scales=v_s[:], in_=v_grouped[(b, h)][:].rearrange("p d t -> p (d t)")
            )
            v_codes[(b, h)], v_scales[(b, h)] = v_c, v_s

        def transpose_qk(b, n):
            qk_ps = psum.tile([P, H, 2, NC, P], BF16, tag="e" if b == 0 and n % 2 else "qk")
            for h in range(H):
                for c in range(NC):
                    chunk = slice(c * P, (c + 1) * P)
                    nc.tensor.matmul(out=qk_ps[:, h, 0, c, :], lhsT=q_sb[b][:, h, n, chunk], rhs=neg_ident[:], start=True, stop=True)
                    nc.tensor.transpose(out=qk_ps[:, h, 1, c, :], in_=k_sb[b][:, h, n, chunk], identity=ident[:])
            qkT_psum[(b, n)] = qk_ps

        def copy_s(b, n):
            if not (n % 2 and b < 2 or n == 1):
                copy_any(b, n, nc.scalar.copy)

        def copy_v(b, n):
            if n % 2 and b < 2 or n == 1:
                copy_any(b, n, nc.vector.tensor_copy)

        def copy_any(b, n, copy):
            if n == 0:
                qkT_b = batches.tile([P, NB, H, 2, NC, P], BF16, tag="qkT")
                qkT[b] = qkT_b
            copy(out=qkT[b][:, n], in_=qkT_psum[(b, n)][:])

        def negated_scores(b, n, h):
            keys = (n + 1) * P
            if n < 2:
                if h == 1:
                    return
                sc = psum_sc.tile([P, H, (n + 1) * P], F32, tag="sc")
                parts = [(h2, sc[:, h2]) for h2 in range(H)]
            else:
                sc = psum_sc.tile([P, S], F32, tag="sc", name="sc")
                parts = [(h, sc[:, :keys])]
            for h2, out_ps in parts:
                by_window = out_ps.rearrange("p (w j) -> p w j", j=P)
                nc.tensor.matmul(out=by_window, lhsT=qkT[b][:, n, h2, 0, 0, :], rhs=qkT[b][:, : n + 1, h2, 1, 0, :], start=True, stop=False)
                nc.tensor.matmul(out=out_ps[:, n * P : keys], lhsT=ident[:], rhs=mask[:], start=False, stop=False)
                nc.tensor.matmul(out=by_window, lhsT=qkT[b][:, n, h2, 0, 1, :], rhs=qkT[b][:, : n + 1, h2, 1, 1, :], start=False, stop=True)
                scores[(b, n, h2)] = out_ps
            if n < 2:
                scores[(b, n)] = sc[:].rearrange("p h (w j) -> p h w j", j=P)
            else:
                scores[(b, n, h, "w")] = by_window

        def window_minima(b, n, h):
            if h == 0:
                sh = stats.tile([P, H, NB], F32, tag="shift")
                shift[(b, n)] = sh
            if n < 2:
                if h == 0:
                    nc.vector.tensor_reduce(out=shift[(b, n)][:, :, : n + 1], in_=scores[(b, n)], axis=AXIS_X, op=ALU.min)
            else:
                nc.vector.tensor_reduce(out=shift[(b, n)][:, h, : n + 1], in_=scores[(b, n, h, "w")], axis=AXIS_X, op=ALU.min)

        def first_exp(b, n, h):
            if h == 0:
                ex_n = blocks.tile([P, H, NB, P], F32, tag="ex")
                ws = stats.tile([P, H, NB], F32, tag="win_sum")
                ex[(b, n)], win_sum[(b, n)] = ex_n, ws
            for w in range(n + 1):
                nc.scalar.activation(
                    out=ex[(b, n)][:, h, w, :], in_=scores[(b, n, h)][:, w * P : (w + 1) * P], func=ACT.Exp,
                    scale=-1.0, bias=shift[(b, n)][:, h, w : w + 1], accum_out=win_sum[(b, n)][:, h, w : w + 1],
                )

        def invert_window_sums(b, n):
            wi = stats.tile([P, H, NB], F32, tag="win_inv")
            nc.vector.reciprocal(out=wi[:, :, : n + 1], in_=win_sum[(b, n)][:, :, : n + 1])
            win_inv[(b, n)] = wi

        def second_exp(b, n, h):
            for w in range(n + 1):
                nc.scalar.activation(
                    out=e_bf[n][:, h, w, :], in_=ex[(b, n)][:, h, w, :], func=ACT.Exp,
                    scale=win_inv[(b, n)][:, h, w : w + 1], accum_out=e_sums[b % 2][:, n, h, w : w + 1],
                )

        def sum_rows(b, n):
            if b >= FIRST_DIRECT:
                row_sum = stats.tile([P, H], F32, tag="row_sum")
                nc.vector.tensor_reduce(out=row_sum[:], in_=e_sums[b % 2][:, n], axis=AXIS_X, op=ALU.add)
                row_sums[(b, n)] = row_sum
            elif n == NB - 1:
                row_sum_b = stats.tile([P, NB, H], F32, tag="row_sum_b")
                nc.vector.tensor_reduce(out=row_sum_b[:], in_=e_sums[b % 2][:], axis=AXIS_X, op=ALU.add)
                row_sums[b] = row_sum_b

        def parked_rows(b, c):
            first = (NB - 1) * P + c * P // COPIES
            return out[b, first : first + 2, :]

        def invert_row_sums(b, n):
            if b >= FIRST_DIRECT:
                row_inv_n = stats.tile([P, H], F32, tag="row_inv")
                nc.vector.reciprocal(out=row_inv_n[:], in_=row_sums[(b, n)][:])
                row_inv[(b, n)] = row_inv_n
            elif n == NB - 1:
                row_inv_b = stats.tile([P, NB, H], F32, tag="row_inv_b")
                nc.vector.reciprocal(out=row_inv_b[:], in_=row_sums[b][:])
                bc = batches.tile([P, P, NB, H], F32, tag="row_inv_bc")
                for c in range(COPIES):
                    nc.sync.dma_start(
                        out=parked_rows(b, c).rearrange("r (p x) -> (r p) x", x=NB * H), in_=row_inv_b[:].rearrange("p n h -> p (n h)")
                    )
                for c in range(COPIES):
                    readers = slice(c * P // COPIES, (c + 1) * P // COPIES)
                    nc.sync.dma_start(
                        out=bc[readers].rearrange("p j n h -> p (j n h)"),
                        in_=parked_rows(b, c).rearrange("r f -> (r f)").partition_broadcast(P // COPIES),
                    )
                row_inv_bc[b] = bc

        def transpose_words(out_ps, rows):
            words = rows.bitcast(F32)
            for u in range(2):
                nc.tensor.transpose(out=out_ps[:, u, :], in_=words[:, u * P : (u + 1) * P], identity=ident_f32[:])

        def transpose_e(b, n):
            eT_ps = psum.tile([P, H, 2, P], F32, tag="e")
            for h in range(H):
                transpose_words(eT_ps[:, h], e_bf[n][:, h].rearrange("p w j -> p (w j)"))
            eT[(b, n)] = eT_ps

        def group_e(b, n):
            e_g = blocks.tile([P, H * NB * P], BF16, tag="e_grouped", align_bytes=64)
            nc.scalar.copy(
                out=e_g[:].bitcast(F32).rearrange("p (h j u) -> p h j u", h=H, u=2),
                in_=eT[(b, n)][:].rearrange("p h u j -> p h j u"),
            )
            e_grouped[(b, n)] = e_g

        def quantise_e(b, n):
            e_c = e_pool.tile([P, H * P], U32, tag="e_codes", align_bytes=64)
            e_s = e_pool.tile([P, H * P], U8, tag="e_scales", align_bytes=64)
            nc.vector.quantize_mx(out=e_c[:].bitcast(FP8X4), scales=e_s[:], in_=e_grouped[(b, n)][:])
            e_codes[(b, n)], e_scales[(b, n)] = e_c, e_s

        def e_times_v(b, n):
            if b >= FIRST_DIRECT:
                av_ps = psum.tile([P, H, DK], F32, tag="mx", bufs=4)
                for h in range(H):
                    cols = slice(h * P, (h + 1) * P)
                    nc.tensor.matmul_mx(
                        out=av_ps[:, h, :],
                        lhsT=e_codes[(b, n)][:, cols].bitcast(FP8X4), lhsT_scale=e_scales[(b, n)][:, cols],
                        rhs=v_codes[(b, h)][:].bitcast(FP8X4), rhs_scale=v_scales[(b, h)][:],
                        start=True, stop=True,
                    )
            else:
                av_ps = psum.tile([P, H * NC, P], F32, tag="mx", bufs=4)
                for h in range(H):
                    cols = slice(h * P, (h + 1) * P)
                    for c in range(NC):
                        chunk = slice(c * P, (c + 1) * P)
                        nc.tensor.matmul_mx(
                            out=av_ps[:, NC * h + c, :],
                            lhsT=v_codes[(b, h)][:, chunk].bitcast(FP8X4), lhsT_scale=v_scales[(b, h)][:, chunk],
                            rhs=e_codes[(b, n)][:, cols].bitcast(FP8X4), rhs_scale=e_scales[(b, n)][:, cols],
                            start=True, stop=True,
                        )
            av[(b, n)] = av_ps

        def divide_transposed(b, n):
            if b < FIRST_DIRECT:
                r_g = blocks.tile([P, P, H, NC], BF16, tag="rows_grouped", align_bytes=64)
                nc.vector.tensor_tensor(
                    out=r_g[:], in0=av[(b, n)][:].rearrange("p (h c) j -> p j h c", h=H),
                    in1=row_inv_bc[b][:, :, n, :].unsqueeze(3).to_broadcast([P, P, H, NC]), op=ALU.mult,
                )
                rows_grouped[(b, n)] = r_g[:].rearrange("p j h c -> p (j h c)")

        def divide_direct(b, n):
            if b >= FIRST_DIRECT:
                a_n = blocks.tile([P, D], BF16, tag="a_bf")
                for h in range(H):
                    nc.scalar.activation(
                        out=a_n[:, h * DK : (h + 1) * DK], in_=av[(b, n)][:, h, :],
                        func=ACT.Copy, scale=row_inv[(b, n)][:, h : h + 1],
                    )
                a_bf[(b, n)] = a_n

        WO = B

        def transpose_rows(b, n):
            if b >= FIRST_DIRECT:
                rows_ps = psum.tile([P, D // P, P], BF16, tag="mx", bufs=4)
                for t in range(D // P):
                    feats = slice(t * P, (t + 1) * P)
                    nc.tensor.transpose(
                        out=rows_ps[:, t, :], in_=wo_sb[:, n, feats] if b == WO else a_bf[(b, n)][:, feats], identity=ident[:]
                    )
                rows_T[(b, n)] = rows_ps

        def group_rows(b, n):
            if b >= FIRST_DIRECT:
                r_g = blocks.tile([P, P, H * NC], BF16, tag="rows_grouped", align_bytes=64, name="r_g")
                (nc.scalar.copy if b < B else nc.vector.tensor_copy)(out=r_g[:], in_=rows_T[(b, n)][:].rearrange("p t j -> p j t"))
                rows_grouped[(b, n)] = r_g[:].rearrange("p j t -> p (j t)")

        def quantise_rows(b, n):
            if b == WO:
                cols = slice(n * P, (n + 1) * P)
                codes, scales = wo_codes[:, cols], wo_scales[:, cols]
            else:
                a_c = blocks.tile([P, P], U32, tag="a_codes", align_bytes=64)
                a_s = blocks.tile([P, P], U8, tag="a_scales", align_bytes=64)
                a_codes[(b, n)], a_scales[(b, n)] = a_c, a_s
                codes, scales = a_c[:], a_s[:]
            nc.vector.quantize_mx(out=codes.bitcast(FP8X4), scales=scales, in_=rows_grouped[(b, n)])

        def project(b, n):
            o_ps = psum.tile([P, D], F32, tag="mx", bufs=4)
            nc.tensor.matmul_mx(
                out=o_ps[:],
                lhsT=a_codes[(b, n)][:].bitcast(FP8X4), lhsT_scale=a_scales[(b, n)][:],
                rhs=wo_codes[:].bitcast(FP8X4), rhs_scale=wo_scales[:],
                start=True, stop=True,
            )
            proj[(b, n)] = o_ps

        def add_bias_and_store(b, n):
            o_sb = outs.tile([P, D], F32, tag="o_sb")
            nc.vector.tensor_tensor(out=o_sb[:], in0=proj[(b, n)][:], in1=bias_bc[:], op=ALU.add)
            nc.sync.dma_start(out=out[b, n * P : (n + 1) * P, :], in_=o_sb[:])

        def load_ahead(b, n):
            if n == 0 and b + 2 < B:
                load_batch(b + 2)

        def exp1(b, n):
            for h in range(H):
                first_exp(b, n, h)

        def exp2(b, n):
            for h in range(H):
                second_exp(b, n, h)

        def sc0(b, n):
            negated_scores(b, n, 0)

        def sc1(b, n):
            negated_scores(b, n, 1)

        def min0(b, n):
            window_minima(b, n, 0)

        def min1(b, n):
            window_minima(b, n, 1)

        def vgroup(b, n):
            if n in (0, 1):
                group_v(b, n)

        def vquant(b, n):
            if n in (0, 1):
                quantise_v(b, n)

        def wo_t(b, n):
            if b == 0:
                transpose_rows(WO, n)

        def wo_g(b, n):
            if b == 0:
                group_rows(WO, n)

        def wo_q(b, n):
            if b == 0:
                quantise_rows(WO, n)

        order = [(b, n) for b in range(B) for n in range(NB)]
        stages = [
            (invert_window_sums, 1, 1),
            (transpose_qk, -2, -2),
            (load_ahead, -1, -1),
            (vgroup, 1, 1),
            (divide_transposed, 8, 99),
            (add_bias_and_store, 9, 99),
            (transpose_rows, 99, 6),
            (wo_t, 2, 2),
            (sc0, -1, -1),
            (quantise_rows, 8, 7),
            (copy_v, -2, -2),
            (transpose_e, 2, 2),
            (sc1, -1, -1),
            (sum_rows, 2, 2),
            (add_bias_and_store, 99, 8),
            (e_times_v, 7, 99),
            (exp1, 0, 0),
            (project, 8, 99),
            (vquant, 4, 3),
            (invert_row_sums, 2, 3),
            (copy_s, -2, -2),
            (min0, -1, -1),
            (wo_g, 3, 3),
            (quantise_e, 4, 99),
            (divide_direct, 99, 5),
            (project, 99, 7),
            (e_times_v, 99, 4),
            (group_rows, 99, 6),
            (exp2, 1, 1),
            (quantise_e, 99, 3),
            (min1, -1, -1),
            (wo_q, 4, 4),
            (group_e, 2, 2),
        ]
        steps = range(-3, len(order) + 14)
        with tc.manual_schedule():
            for step in steps:
                for stage, lag, lag_direct in stages:
                    for b, n in order:
                        if step - (lag_direct if b >= FIRST_DIRECT else lag) == b * NB + n:
                            stage(b, n)
